import numpy as np
import ml_dtypes


def mxq(x, axis, fmt="e4m3"):
    dtype, down = {"e4m3": (ml_dtypes.float8_e4m3fn, 7), "e5m2": (ml_dtypes.float8_e5m2, 14)}[fmt]
    v = np.moveaxis(np.asarray(x, np.float32).astype(ml_dtypes.bfloat16).astype(np.float64), axis, -1)
    blocks = v.reshape(v.shape[:-1] + (-1, 32))
    amax = np.abs(blocks).max(-1, keepdims=True)
    byte = np.maximum(np.where(amax > 0, np.frexp(amax)[1] - 1 + 127, 0) - down, 1)
    scale = np.exp2(byte - 127.0)
    codes = (blocks / scale).astype(np.float32).astype(dtype).astype(np.float64)
    return np.moveaxis((codes * scale).reshape(v.shape), -1, axis)


WIDE = False


def mx_kscale(k):
    if not WIDE:
        return np.ones(k)
    levels = np.array([10, -10, 5, -5, 0])
    a = np.random.permutation(np.resize(levels, k // 512 * 4)).reshape(k // 512, 4)
    idx = np.arange(k)
    return np.exp2(a[idx // 512, idx % 128 // 32])


BF16 = ml_dtypes.bfloat16


def bf(x):
    return np.asarray(x, np.float32).astype(BF16)


def f64(x):
    return np.asarray(x).astype(np.float64)


I, H, B = 2048, 2048, 128


def sigmoid(v):
    return 1.0 / (1.0 + np.exp(-v))


def setup_inputs():
    s, t = mx_kscale(I), mx_kscale(H)
    d = {"x": bf(np.random.standard_normal((I, B)) * s[:, None]), "h": bf(np.random.standard_normal((B, H)) * t[None, :]),
         "c": bf(np.random.standard_normal((B, H))), "ig": bf(np.random.standard_normal((H, B)) * 0.35)}
    for n in ("w_if", "w_io"):
        d[n] = bf(np.random.standard_normal((H, I)) * 0.7 / np.sqrt(I) / s[None, :])
    for n in ("w_hf", "w_ho"):
        d[n] = bf(np.random.standard_normal((H, H)) * 0.7 / np.sqrt(H) / t[None, :])
    for n in ("b_if", "b_hf", "b_io", "b_ho"):
        d[n] = bf(np.random.standard_normal((H, 1)) * 0.3)
    return d


def reference(x, h, c, ig, w_if, w_io, w_hf, w_ho, b_if, b_hf, b_io, b_ho):
    xq = mxq(f64(x), 0, "e4m3")
    hq = mxq(f64(h).T, 0, "e4m3")
    f = sigmoid((mxq(f64(w_if), 1, "e4m3") @ xq) + f64(b_if) + (mxq(f64(w_hf), 1, "e4m3") @ hq) + f64(b_hf))
    o = sigmoid((mxq(f64(w_io), 1, "e4m3") @ xq) + f64(b_io) + (mxq(f64(w_ho), 1, "e4m3") @ hq) + f64(b_ho))
    c_next_t = f * f64(c).T + f64(ig)
    h_next_t = o * np.tanh(c_next_t)
    return h_next_t.T, c_next_t.T

@@ -1,0 +1,274 @@
+from contextlib import ExitStack
+
+import concourse.mybir as mybir
+from concourse.masks import make_identity
+
+F32 = mybir.dt.float32
+BF16 = mybir.dt.bfloat16
+U32 = mybir.dt.uint32
+U8 = mybir.dt.uint8
+I32 = mybir.dt.int32
+FP8X4 = mybir.dt.float8_e4m3fn_x4
+ACT = mybir.ActivationFunctionType
+ALU = mybir.AluOpType
+
+P = 128
+K = 2048
+HID = 2048
+NCOL = 512
+NCHUNK = 16
+NPASS = 64
+WBUFS = 6
+UNIT = 4
+COPY_ENGINES = "SSSVSSSV"
+
+FLOPS = 2 * 4 * 2048 * 2048 * 128
+
+
+def tile_naivelstm_pb_kernel(
+    tc, x, h, c, ig, w_if, w_io, w_hf, w_ho, b_if, b_hf, b_io, b_ho, out_0, out_1
+):
+    nc = tc.nc
+    with ExitStack() as ctx:
+        ctx.enter_context(tc.manual_schedule())
+        const = ctx.enter_context(tc.tile_pool(name="const", bufs=1))
+        wpool = ctx.enter_context(tc.tile_pool(name="wpool", bufs=WBUFS))
+        gpool = ctx.enter_context(tc.tile_pool(name="gpool", bufs=5))
+        cpool = ctx.enter_context(tc.tile_pool(name="cpool", bufs=10))
+        ep = ctx.enter_context(tc.tile_pool(name="ep", bufs=2))
+        accp = ctx.enter_context(tc.psum_pool(name="accp", bufs=1))
+        tp = ctx.enter_context(tc.psum_pool(name="tp", bufs=6))
+
+        w_views = [
+            w.rearrange("(a q j) k -> a q (j k)", a=4, q=P, j=4)
+            for w in (w_if, w_hf, w_io, w_ho)
+        ]
+
+        ident32 = const.tile([P, P], F32, name="ident32")
+        identb = const.tile([P, P], BF16, name="identb")
+        ones = const.tile([P, P], BF16, name="ones")
+        brow = const.tile([P, 2 * HID], BF16, name="brow")
+        nc.vector.memset(brow[:].bitcast(I32), 0)
+        make_identity(nc, ident32[:])
+        make_identity(nc, identb[:])
+        nc.gpsimd.memset(ones[:], 1.0)
+        warm = const.tile([P, 2], F32, name="warm")
+        nc.vector.memset(warm[:], 0.0)
+        nc.scalar.activation(out=warm[:, 1:2], in_=warm[:, 0:1], func=ACT.Sigmoid)
+
+        h_sb = const.tile([P, K], BF16, name="h_sb")
+        nc.sync.dma_start(out=h_sb[:], in_=h)
+        xraw = const.tile([P, 8, 2, P], BF16, name="xraw")
+        nc.sync.dma_start(out=xraw[:], in_=x.rearrange("(s p e) b -> p s e b", s=8, p=P, e=2))
+        ig_sb = const.tile([P, 4, 4 * P], BF16, name="ig_sb")
+        nc.sync.dma_start(out=ig_sb[:], in_=ig.rearrange("(a q j) b -> q a (j b)", a=4, q=P, j=4))
+        for row, gate, b in ((0, 0, b_if), (1, 0, b_hf), (0, 1, b_io), (1, 1, b_ho)):
+            nc.scalar.dma_start(
+                out=brow[row : row + 1, gate * HID : (gate + 1) * HID],
+                in_=b.rearrange("n o -> o n"),
+            )
+        c_sb = const.tile([P, HID], BF16, name="c_sb")
+
+        wt = {}
+
+        def load(ci):
+            t = wpool.tile([P, 4 * K], BF16, name="wt", tag="wt")
+            nc.sync.dma_start(out=t[:], in_=w_views[ci % 4][ci // 4, :, :])
+            wt[ci] = t
+
+        for ci in range(WBUFS):
+            load(ci)
+            if ci == 1:
+                nc.sync.dma_start(out=c_sb[:], in_=c)
+
+        def transpose_bank(src32, cols):
+            bank = tp.tile([P, 2, 2, P], F32, name="xt", tag="xt")
+            for u in range(2):
+                for s in range(2):
+                    col = cols[u][s]
+                    nc.tensor.transpose(bank[:, u, s, :], src32[:, col : col + P], ident32[:])
+            return bank
+
+        def copy_bank(eng, grouped, half, bank):
+            dst = grouped[:].bitcast(F32).rearrange("p (n u) -> p n u", u=2)
+            dst = dst[:, half * 256 : (half + 1) * 256, :]
+            src = bank[:].rearrange("p u s q -> p (s q) u")
+            if eng == "S":
+                nc.scalar.copy(out=dst, in_=src)
+            else:
+                nc.vector.tensor_copy(out=dst, in_=src)
+
+        def quantise(grouped, codes, scales):
+            nc.vector.quantize_mx(out=codes[:].bitcast(FP8X4), scales=scales[:], in_=grouped[:])
+
+        h32 = h_sb[:].bitcast(F32)
+        hg = const.tile([P, K], BF16, name="hg", align_bytes=64)
+        hbanks = []
+        for gp in range(2):
+            hbanks.append(
+                transpose_bank(h32, [[(2 * (2 * gp + s) + u) * P for s in range(2)] for u in range(2)])
+            )
+        copy_bank("S", hg, 0, hbanks[0])
+        copy_bank("V", hg, 1, hbanks[1])
+
+        xg = const.tile([P, 4, P, 4], BF16, name="xg", align_bytes=64)
+        nc.vector.tensor_copy(
+            out=xg[:], in_=xraw[:].rearrange("p (g u) e b -> p g b (u e)", g=4, u=2)
+        )
+        act_codes = []
+        act_scales = []
+        for nm in ("x", "h"):
+            act_codes.append(const.tile([P, 512], U32, name="codes_" + nm, align_bytes=64))
+            act_scales.append(const.tile([P, 512], U8, name="scales_" + nm, align_bytes=64))
+        nc.vector.quantize_mx(
+            out=act_codes[1][:].bitcast(FP8X4), scales=act_scales[1][:], in_=hg[:]
+        )
+        nc.vector.quantize_mx(
+            out=act_codes[0][:].bitcast(FP8X4),
+            scales=act_scales[0][:],
+            in_=xg[:].rearrange("p g b t -> p (g b t)"),
+        )
+
+        igT = const.tile([P, 4, 4, P], BF16, name="igT")
+        for half in range(2):
+            ibank = tp.tile([P, 2, 4, P], BF16, name="ibank", tag="xt")
+            for a2 in range(2):
+                for j in range(4):
+                    nc.tensor.transpose(
+                        ibank[:, a2, j, :],
+                        ig_sb[:, 2 * half + a2, j * P : (j + 1) * P],
+                        identb[:],
+                    )
+            if half == 0:
+                nc.scalar.copy(out=igT[:, 0:2, :, :], in_=ibank[:])
+            else:
+                nc.vector.tensor_copy(out=igT[:, 2:4, :, :], in_=ibank[:])
+
+        bias = const.tile([P, 2 * HID], F32, name="bias")
+        for n in range(8):
+            bbank = tp.tile([P, NCOL], F32, name="bbank", tag="xt")
+            nc.tensor.matmul(
+                out=bbank[:], lhsT=ones[:], rhs=brow[:, n * NCOL : (n + 1) * NCOL], start=True, stop=True
+            )
+            if n % 2 == 0:
+                nc.scalar.copy(out=bias[:, n * NCOL : (n + 1) * NCOL], in_=bbank[:])
+            else:
+                nc.vector.tensor_copy(out=bias[:, n * NCOL : (n + 1) * NCOL], in_=bbank[:])
+
+        grouped = {}
+        codes = {}
+        scales = {}
+        acc = {}
+        state = {}
+        deferred = {}
+
+        def defer(slot, fn):
+            deferred[slot] = deferred.get(slot, []) + [fn]
+
+        def stage_t(i):
+            ci, g = divmod(i, 4)
+            w32 = wt[ci][:].bitcast(F32)
+            grouped[i] = gpool.tile([P, K], BF16, name="grouped", tag="grouped", align_bytes=64)
+            banks = []
+            for jp in range(2):
+                banks.append(
+                    transpose_bank(
+                        w32,
+                        [[(2 * jp + s) * 1024 + (2 * g + u) * P for s in range(2)] for u in range(2)],
+                    )
+                )
+            for jp in range(2):
+                copy_bank(COPY_ENGINES[(2 * i + jp) % 8], grouped[i], jp, banks[jp])
+
+        def stage_q(i):
+            codes[i] = cpool.tile([P, NCOL], U32, name="codes", tag="codes", align_bytes=64)
+            scales[i] = cpool.tile([P, NCOL], U8, name="scales", tag="scales", align_bytes=64)
+            quantise(grouped[i], codes[i], scales[i])
+
+        def stage_mx(i):
+            ci, g = divmod(i, 4)
+            a, wsel = divmod(ci, 4)
+            gate, opnd = divmod(wsel, 2)
+            if opnd == 0 and g == 0:
+                acc[gate] = accp.tile([P, NCOL], F32, name="acc%d" % gate, tag="acc%d" % gate)
+            nc.tensor.matmul_mx(
+                out=acc[gate][:],
+                lhsT=act_codes[opnd][:, g * P : (g + 1) * P].bitcast(FP8X4),
+                lhsT_scale=act_scales[opnd][:, g * P : (g + 1) * P],
+                rhs=codes[i][:].bitcast(FP8X4),
+                rhs_scale=scales[i][:],
+                start=(opnd == 0 and g == 0),
+                stop=(opnd == 1 and g == 3),
+            )
+
+        def natural(ap):
+            return ap.rearrange("p (q j) -> p q j", j=4)
+
+        def ep_z(a, gate):
+            z = ep.tile([P, NCOL], F32, name="z", tag="z")
+            nc.vector.tensor_tensor(
+                out=natural(z[:]),
+                in0=acc[gate][:].rearrange("p (j q) -> p q j", j=4),
+                in1=natural(bias[:, gate * HID + a * NCOL : gate * HID + (a + 1) * NCOL]),
+                op=ALU.add,
+            )
+            state["z"] = z
+
+        def ep_sig(a, gate):
+            s = ep.tile([P, NCOL], F32, name="sg", tag="sg")
+            nc.scalar.activation(out=s[:], in_=state["z"][:], func=ACT.Sigmoid)
+            state["s"] = s
+
+        def ep_cnext(a):
+            t = ep.tile([P, NCOL], F32, name="fc", tag="fc")
+            nc.vector.tensor_tensor(
+                out=t[:], in0=state["s"][:], in1=c_sb[:, a * NCOL : (a + 1) * NCOL], op=ALU.mult
+            )
+            cn = ep.tile([P, NCOL], F32, name="cn", tag="cn")
+            nc.vector.tensor_tensor(
+                out=natural(cn[:]),
+                in0=natural(t[:]),
+                in1=igT[:, a, :, :].rearrange("p j q -> p q j"),
+                op=ALU.add,
+            )
+            state["cn"] = cn
+
+        def ep_tanh(a):
+            nc.sync.dma_start(out=out_1[:, a * NCOL : (a + 1) * NCOL], in_=state["cn"][:])
+            th = ep.tile([P, NCOL], F32, name="th", tag="th")
+            nc.scalar.activation(out=th[:], in_=state["cn"][:], func=ACT.Tanh)
+            state["th"] = th
+
+        def ep_hnext(a):
+            hn = ep.tile([P, NCOL], F32, name="hn", tag="hn")
+            nc.vector.tensor_tensor(out=hn[:], in0=state["s"][:], in1=state["th"][:], op=ALU.mult)
+            nc.sync.dma_start(out=out_0[:, a * NCOL : (a + 1) * NCOL], in_=hn[:])
+
+        def schedule_epilogue(slot, ci):
+            a, wsel = divmod(ci, 4)
+            if wsel == 1:
+                defer(slot + 1, lambda: ep_z(a, 0))
+                defer(slot + 2, lambda: ep_sig(a, 0))
+                defer(slot + 3, lambda: ep_cnext(a))
+                defer(slot + 4, lambda: ep_tanh(a))
+            if wsel == 3:
+                defer(slot + 1, lambda: ep_z(a, 1))
+                defer(slot + 2, lambda: ep_sig(a, 1))
+                defer(slot + 3, lambda: ep_hnext(a))
+
+        for slot in range(NPASS + UNIT + 8):
+            if slot < NPASS:
+                stage_t(slot)
+                if slot % 4 == 3 and slot // 4 + WBUFS < NCHUNK:
+                    load(slot // 4 + WBUFS)
+            if 0 <= slot - 2 < NPASS:
+                stage_q(slot - 2)
+            if slot % UNIT == UNIT - 1:
+                first = slot + 1 - 2 * UNIT
+                if 0 <= first < NPASS:
+                    for i in range(first, first + UNIT):
+                        stage_mx(i)
+                        if i % 4 == 3:
+                            schedule_epilogue(slot, i // 4)
+            for fn in deferred.get(slot, []):
+                fn()

@@ -16,13 +16,23 @@ P = 128
 K = 2048
 HID = 2048
 NCOL = 512
-NCHUNK = 16
-NPASS = 64
-WBUFS = 6
-UNIT = 4
-COPY_ENGINES = "SSSVSSSV"
+WBUFS = 10
+QLAG = 2
+MXLAG = 6
+V_COPIES = (3, 8, 13)
+EARLY_STORES = 0
+BIAS_AT = (9, 10, 11, 12, 13, 14, 15, 17)
 
 FLOPS = 2 * 4 * 2048 * 2048 * 128
+
+CHUNKS = (
+    (0, 0), (1, 0), (2, 0), (3, 0),
+    (0, 1), (1, 1), (2, 1), (3, 1),
+    (0, 2), (1, 2), (0, 3), (1, 3),
+    (2, 2), (3, 2), (2, 3), (3, 3),
+)
+NCH = len(CHUNKS)
+LAST = NCH - 1
 
 
 def tile_naivelstm_pb_kernel(
@@ -33,14 +43,14 @@ def tile_naivelstm_pb_kernel(
         ctx.enter_context(tc.manual_schedule())
         const = ctx.enter_context(tc.tile_pool(name="const", bufs=1))
         wpool = ctx.enter_context(tc.tile_pool(name="wpool", bufs=WBUFS))
-        gpool = ctx.enter_context(tc.tile_pool(name="gpool", bufs=5))
-        cpool = ctx.enter_context(tc.tile_pool(name="cpool", bufs=10))
+        gpool = ctx.enter_context(tc.tile_pool(name="gpool", bufs=8))
+        cpool = ctx.enter_context(tc.tile_pool(name="cpool", bufs=3))
         ep = ctx.enter_context(tc.tile_pool(name="ep", bufs=2))
         accp = ctx.enter_context(tc.psum_pool(name="accp", bufs=1))
         tp = ctx.enter_context(tc.psum_pool(name="tp", bufs=6))
 
         w_views = [
-            w.rearrange("(a q j) k -> a q (j k)", a=4, q=P, j=4)
+            w.rearrange("(a q s r) k -> a s q (r k)", a=4, q=P, s=2, r=2)
             for w in (w_if, w_hf, w_io, w_ho)
         ]
 
@@ -56,30 +66,52 @@ def tile_naivelstm_pb_kernel(
         nc.vector.memset(warm[:], 0.0)
         nc.scalar.activation(out=warm[:, 1:2], in_=warm[:, 0:1], func=ACT.Sigmoid)
 
+        NLOADS = 2 * LAST + 4
+        wt = {}
+        stores = {"open": False, "early": EARLY_STORES, "pending": []}
+
+        def load(n):
+            if n < 2 * LAST:
+                t = wpool.tile([P, 2 * K], BF16, name="wt", tag="wt")
+                wsel, a = CHUNKS[n // 2]
+                nc.sync.dma_start(out=t[:], in_=w_views[wsel][a, n % 2, :, :])
+            else:
+                j = n - 2 * LAST
+                t = wpool.tile([P, K], BF16, name="wt", tag="wt")
+                nc.sync.dma_start(out=t[:], in_=w_ho[3 * NCOL + j * P : 3 * NCOL + (j + 1) * P, :])
+            wt[n] = t
+            if n == NLOADS - 1:
+                stores["open"] = True
+                for dst, src in stores["pending"]:
+                    nc.sync.dma_start(out=dst, in_=src)
+
+        def store(dst, src):
+            if stores["open"] or stores["early"] > 0:
+                stores["early"] = stores["early"] - 1
+                nc.sync.dma_start(out=dst, in_=src)
+            else:
+                stores["pending"].append((dst, src))
+
         h_sb = const.tile([P, K], BF16, name="h_sb")
-        nc.sync.dma_start(out=h_sb[:], in_=h)
         xraw = const.tile([P, 8, 2, P], BF16, name="xraw")
-        nc.sync.dma_start(out=xraw[:], in_=x.rearrange("(s p e) b -> p s e b", s=8, p=P, e=2))
         ig_sb = const.tile([P, 4, 4 * P], BF16, name="ig_sb")
-        nc.sync.dma_start(out=ig_sb[:], in_=ig.rearrange("(a q j) b -> q a (j b)", a=4, q=P, j=4))
+        c_sb = const.tile([P, HID], BF16, name="c_sb")
         for row, gate, b in ((0, 0, b_if), (1, 0, b_hf), (0, 1, b_io), (1, 1, b_ho)):
             nc.scalar.dma_start(
                 out=brow[row : row + 1, gate * HID : (gate + 1) * HID],
                 in_=b.rearrange("n o -> o n"),
             )
-        c_sb = const.tile([P, HID], BF16, name="c_sb")
-
-        wt = {}
-
-        def load(ci):
-            t = wpool.tile([P, 4 * K], BF16, name="wt", tag="wt")
-            nc.sync.dma_start(out=t[:], in_=w_views[ci % 4][ci // 4, :, :])
-            wt[ci] = t
-
-        for ci in range(WBUFS):
-            load(ci)
-            if ci == 1:
-                nc.sync.dma_start(out=c_sb[:], in_=c)
+        load(0)
+        nc.sync.dma_start(out=xraw[:], in_=x.rearrange("(s p e) b -> p s e b", s=8, p=P, e=2))
+        load(1)
+        nc.sync.dma_start(out=h_sb[:], in_=h)
+        load(2)
+        load(3)
+        nc.sync.dma_start(out=ig_sb[:], in_=ig.rearrange("(a q j) b -> q a (j b)", a=4, q=P, j=4))
+        load(4)
+        nc.sync.dma_start(out=c_sb[:], in_=c)
+        for n in range(5, WBUFS):
+            load(n)
 
         def transpose_bank(src32, cols):
             bank = tp.tile([P, 2, 2, P], F32, name="xt", tag="xt")
@@ -89,117 +121,127 @@ def tile_naivelstm_pb_kernel(
                     nc.tensor.transpose(bank[:, u, s, :], src32[:, col : col + P], ident32[:])
             return bank
 
-        def copy_bank(eng, grouped, half, bank):
+        def copy_bank(eng, bank):
+            grouped = gpool.tile([P, K // 2], BF16, name="grouped", tag="grouped", align_bytes=64)
             dst = grouped[:].bitcast(F32).rearrange("p (n u) -> p n u", u=2)
-            dst = dst[:, half * 256 : (half + 1) * 256, :]
             src = bank[:].rearrange("p u s q -> p (s q) u")
             if eng == "S":
                 nc.scalar.copy(out=dst, in_=src)
             else:
                 nc.vector.tensor_copy(out=dst, in_=src)
+            return grouped
 
         def quantise(grouped, codes, scales):
-            nc.vector.quantize_mx(out=codes[:].bitcast(FP8X4), scales=scales[:], in_=grouped[:])
+            nc.vector.quantize_mx(out=codes.bitcast(FP8X4), scales=scales, in_=grouped[:])
 
-        h32 = h_sb[:].bitcast(F32)
-        hg = const.tile([P, K], BF16, name="hg", align_bytes=64)
-        hbanks = []
-        for gp in range(2):
-            hbanks.append(
-                transpose_bank(h32, [[(2 * (2 * gp + s) + u) * P for s in range(2)] for u in range(2)])
-            )
-        copy_bank("S", hg, 0, hbanks[0])
-        copy_bank("V", hg, 1, hbanks[1])
+        def row_block_cols(gp):
+            return [[(2 * (2 * gp + s) + u) * P for s in range(2)] for u in range(2)]
 
-        xg = const.tile([P, 4, P, 4], BF16, name="xg", align_bytes=64)
-        nc.vector.tensor_copy(
-            out=xg[:], in_=xraw[:].rearrange("p (g u) e b -> p g b (u e)", g=4, u=2)
-        )
         act_codes = []
         act_scales = []
         for nm in ("x", "h"):
             act_codes.append(const.tile([P, 512], U32, name="codes_" + nm, align_bytes=64))
             act_scales.append(const.tile([P, 512], U8, name="scales_" + nm, align_bytes=64))
-        nc.vector.quantize_mx(
-            out=act_codes[1][:].bitcast(FP8X4), scales=act_scales[1][:], in_=hg[:]
-        )
-        nc.vector.quantize_mx(
-            out=act_codes[0][:].bitcast(FP8X4),
-            scales=act_scales[0][:],
-            in_=xg[:].rearrange("p g b t -> p (g b t)"),
-        )
+
+        def prepare_x():
+            xg = const.tile([P, K], BF16, name="xg", align_bytes=64)
+            nc.vector.tensor_copy(
+                out=xg[:].rearrange("p (g b t) -> p g b t", g=4, b=P, t=4),
+                in_=xraw[:].rearrange("p (g u) e b -> p g b (u e)", g=4, u=2),
+            )
+            return xg
+
+        def prepare_h():
+            h32 = h_sb[:].bitcast(F32)
+            hbanks = [transpose_bank(h32, row_block_cols(gp)) for gp in range(2)]
+            return [copy_bank("SV"[gp], hbanks[gp]) for gp in range(2)]
 
         igT = const.tile([P, 4, 4, P], BF16, name="igT")
-        for half in range(2):
-            ibank = tp.tile([P, 2, 4, P], BF16, name="ibank", tag="xt")
-            for a2 in range(2):
-                for j in range(4):
-                    nc.tensor.transpose(
-                        ibank[:, a2, j, :],
-                        ig_sb[:, 2 * half + a2, j * P : (j + 1) * P],
-                        identb[:],
-                    )
-            if half == 0:
-                nc.scalar.copy(out=igT[:, 0:2, :, :], in_=ibank[:])
-            else:
-                nc.vector.tensor_copy(out=igT[:, 2:4, :, :], in_=ibank[:])
+
+        def prepare_ig():
+            for half in range(2):
+                ibank = tp.tile([P, 2, 4, P], BF16, name="ibank", tag="xt")
+                for a2 in range(2):
+                    for j in range(4):
+                        nc.tensor.transpose(
+                            ibank[:, a2, j, :],
+                            ig_sb[:, 2 * half + a2, j * P : (j + 1) * P],
+                            identb[:],
+                        )
+                nc.scalar.copy(out=igT[:, 2 * half : 2 * half + 2, :, :], in_=ibank[:])
 
         bias = const.tile([P, 2 * HID], F32, name="bias")
-        for n in range(8):
-            bbank = tp.tile([P, NCOL], F32, name="bbank", tag="xt")
-            nc.tensor.matmul(
-                out=bbank[:], lhsT=ones[:], rhs=brow[:, n * NCOL : (n + 1) * NCOL], start=True, stop=True
-            )
-            if n % 2 == 0:
-                nc.scalar.copy(out=bias[:, n * NCOL : (n + 1) * NCOL], in_=bbank[:])
-            else:
-                nc.vector.tensor_copy(out=bias[:, n * NCOL : (n + 1) * NCOL], in_=bbank[:])
 
+        def spread_bias(gate, a):
+            cols = slice(gate * HID + a * NCOL, gate * HID + (a + 1) * NCOL)
+            bbank = tp.tile([P, NCOL], F32, name="bbank", tag="xt")
+            nc.tensor.matmul(out=bbank[:], lhsT=ones[:], rhs=brow[:, cols], start=True, stop=True)
+            nc.scalar.copy(out=bias[:, cols], in_=bbank[:])
+
+        cn_all = const.tile([P, HID], F32, name="cn_all")
+        hn_all = const.tile([P, HID], F32, name="hn_all")
         grouped = {}
         codes = {}
         scales = {}
         acc = {}
         state = {}
+        th = {}
+        blk = {}
         deferred = {}
 
         def defer(slot, fn):
             deferred[slot] = deferred.get(slot, []) + [fn]
 
-        def stage_t(i):
-            ci, g = divmod(i, 4)
-            w32 = wt[ci][:].bitcast(F32)
-            grouped[i] = gpool.tile([P, K], BF16, name="grouped", tag="grouped", align_bytes=64)
-            banks = []
-            for jp in range(2):
-                banks.append(
-                    transpose_bank(
-                        w32,
-                        [[(2 * jp + s) * 1024 + (2 * g + u) * P for s in range(2)] for u in range(2)],
-                    )
-                )
-            for jp in range(2):
-                copy_bank(COPY_ENGINES[(2 * i + jp) % 8], grouped[i], jp, banks[jp])
+        def unit_t(n, eng):
+            ci, r = divmod(n, 8)
+            first, second = divmod(r, 4) if ci < LAST else divmod(r, 2)
+            if ci < LAST:
+                w32 = wt[2 * ci + first][:].bitcast(F32)
+                cols = [[s * 1024 + (2 * second + u) * P for s in range(2)] for u in range(2)]
+            else:
+                w32 = wt[2 * LAST + first][:].bitcast(F32)
+                cols = row_block_cols(second)
+            grouped[n] = copy_bank(eng, transpose_bank(w32, cols))
 
-        def stage_q(i):
-            codes[i] = cpool.tile([P, NCOL], U32, name="codes", tag="codes", align_bytes=64)
-            scales[i] = cpool.tile([P, NCOL], U8, name="scales", tag="scales", align_bytes=64)
-            quantise(grouped[i], codes[i], scales[i])
+        def unit_q(n):
+            ci, r = divmod(n, 8)
+            if r == 0:
+                codes[ci] = cpool.tile([P, 4, NCOL], U32, name="codes", tag="codes", align_bytes=64)
+                scales[ci] = cpool.tile([P, 4, NCOL], U8, name="scales", tag="scales", align_bytes=64)
+            if ci < LAST:
+                half, row = divmod(r, 4)
+            else:
+                row, half = divmod(r, 2)
+            cols = slice(half * 256, (half + 1) * 256)
+            quantise(grouped[n], codes[ci][:, row, cols], scales[ci][:, row, cols])
 
-        def stage_mx(i):
-            ci, g = divmod(i, 4)
-            a, wsel = divmod(ci, 4)
-            gate, opnd = divmod(wsel, 2)
-            if opnd == 0 and g == 0:
-                acc[gate] = accp.tile([P, NCOL], F32, name="acc%d" % gate, tag="acc%d" % gate)
+        def mx(out, opnd, g, ci, row, cols, start, stop):
             nc.tensor.matmul_mx(
-                out=acc[gate][:],
+                out=out,
                 lhsT=act_codes[opnd][:, g * P : (g + 1) * P].bitcast(FP8X4),
                 lhsT_scale=act_scales[opnd][:, g * P : (g + 1) * P],
-                rhs=codes[i][:].bitcast(FP8X4),
-                rhs_scale=scales[i][:],
-                start=(opnd == 0 and g == 0),
-                stop=(opnd == 1 and g == 3),
+                rhs=codes[ci][:, row, cols].bitcast(FP8X4),
+                rhs_scale=scales[ci][:, row, cols],
+                start=start,
+                stop=stop,
             )
+
+        def chunk_mx(ci):
+            wsel, a = CHUNKS[ci]
+            gate, opnd = divmod(wsel, 2)
+            alone = (wsel, a) == (2, 3)
+            if opnd == 0:
+                acc[gate] = accp.tile([P, NCOL], F32, name="acc%d" % gate, tag="acc%d" % gate)
+            for g in range(4):
+                mx(acc[gate][:], opnd, g, ci, g, slice(0, NCOL), opnd == 0 and g == 0, (opnd == 1 or alone) and g == 3)
+
+        def block_mx(j):
+            if j < 2:
+                blk[j] = accp.tile([P, P], F32, name="acc%d" % j, tag="acc%d" % j)
+            else:
+                blk[j] = tp.tile([P, P], F32, name="blk", tag="xt")
+            for g in range(4):
+                mx(blk[j][:], 1, g, LAST, j, slice(g * P, (g + 1) * P), g == 0, g == 3)
 
         def natural(ap):
             return ap.rearrange("p (q j) -> p q j", j=4)
@@ -214,61 +256,150 @@ def tile_naivelstm_pb_kernel(
             )
             state["z"] = z
 
-        def ep_sig(a, gate):
+        def ep_sig():
             s = ep.tile([P, NCOL], F32, name="sg", tag="sg")
             nc.scalar.activation(out=s[:], in_=state["z"][:], func=ACT.Sigmoid)
             state["s"] = s
 
         def ep_cnext(a):
+            cols = slice(a * NCOL, (a + 1) * NCOL)
             t = ep.tile([P, NCOL], F32, name="fc", tag="fc")
+            nc.vector.tensor_tensor(out=t[:], in0=state["s"][:], in1=c_sb[:, cols], op=ALU.mult)
             nc.vector.tensor_tensor(
-                out=t[:], in0=state["s"][:], in1=c_sb[:, a * NCOL : (a + 1) * NCOL], op=ALU.mult
-            )
-            cn = ep.tile([P, NCOL], F32, name="cn", tag="cn")
-            nc.vector.tensor_tensor(
-                out=natural(cn[:]),
+                out=natural(cn_all[:, cols]),
                 in0=natural(t[:]),
                 in1=igT[:, a, :, :].rearrange("p j q -> p q j"),
                 op=ALU.add,
             )
-            state["cn"] = cn
 
         def ep_tanh(a):
-            nc.sync.dma_start(out=out_1[:, a * NCOL : (a + 1) * NCOL], in_=state["cn"][:])
-            th = ep.tile([P, NCOL], F32, name="th", tag="th")
-            nc.scalar.activation(out=th[:], in_=state["cn"][:], func=ACT.Tanh)
-            state["th"] = th
+            cols = slice(a * NCOL, (a + 1) * NCOL)
+            store(out_1[:, cols], cn_all[:, cols])
+            th[a] = ep.tile([P, NCOL], F32, name="th", tag="th")
+            nc.scalar.activation(out=th[a][:], in_=cn_all[:, cols], func=ACT.Tanh)
 
         def ep_hnext(a):
-            hn = ep.tile([P, NCOL], F32, name="hn", tag="hn")
-            nc.vector.tensor_tensor(out=hn[:], in0=state["s"][:], in1=state["th"][:], op=ALU.mult)
-            nc.sync.dma_start(out=out_0[:, a * NCOL : (a + 1) * NCOL], in_=hn[:])
+            cols = slice(a * NCOL, (a + 1) * NCOL)
+            nc.vector.tensor_tensor(out=hn_all[:, cols], in0=state["s"][:], in1=th[a][:], op=ALU.mult)
+            store(out_0[:, cols], hn_all[:, cols])
+
+        def keep_zpart():
+            state["zpart"] = state["z"]
 
         def schedule_epilogue(slot, ci):
-            a, wsel = divmod(ci, 4)
+            wsel, a = CHUNKS[ci]
             if wsel == 1:
                 defer(slot + 1, lambda: ep_z(a, 0))
-                defer(slot + 2, lambda: ep_sig(a, 0))
-                defer(slot + 3, lambda: ep_cnext(a))
-                defer(slot + 4, lambda: ep_tanh(a))
+                defer(slot + 3, ep_sig)
+                defer(slot + 5, lambda: ep_cnext(a))
+                defer(slot + 7, lambda: ep_tanh(a))
             if wsel == 3:
                 defer(slot + 1, lambda: ep_z(a, 1))
-                defer(slot + 2, lambda: ep_sig(a, 1))
-                defer(slot + 3, lambda: ep_hnext(a))
+                defer(slot + 3, ep_sig)
+                defer(slot + 5, lambda: ep_hnext(a))
+            if (wsel, a) == (2, 3):
+                defer(slot + 1, lambda: ep_z(a, 1))
+                defer(slot + 1, keep_zpart)
 
-        for slot in range(NPASS + UNIT + 8):
-            if slot < NPASS:
-                stage_t(slot)
-                if slot % 4 == 3 and slot // 4 + WBUFS < NCHUNK:
-                    load(slot // 4 + WBUFS)
-            if 0 <= slot - 2 < NPASS:
-                stage_q(slot - 2)
-            if slot % UNIT == UNIT - 1:
-                first = slot + 1 - 2 * UNIT
-                if 0 <= first < NPASS:
-                    for i in range(first, first + UNIT):
-                        stage_mx(i)
-                        if i % 4 == 3:
-                            schedule_epilogue(slot, i // 4)
-            for fn in deferred.get(slot, []):
+        def last_z(j):
+            zl = ep.tile([P, P], F32, name="zl", tag="zl", bufs=4)
+            nc.vector.tensor_tensor(
+                out=zl[:], in0=blk[j][:], in1=state["zpart"][:, j * P : (j + 1) * P], op=ALU.add
+            )
+            state["zl%d" % j] = zl
+
+        def last_sig(j):
+            sl = ep.tile([P, P], F32, name="sl", tag="sl", bufs=4)
+            nc.scalar.activation(out=sl[:], in_=state["zl%d" % j][:], func=ACT.Sigmoid)
+            state["sl%d" % j] = sl
+
+        def last_h(j):
+            cols = slice(3 * NCOL + j * P, 3 * NCOL + (j + 1) * P)
+            nc.vector.tensor_tensor(
+                out=hn_all[:, cols], in0=state["sl%d" % j][:], in1=th[3][:, j * P : (j + 1) * P], op=ALU.mult
+            )
+            store(out_0[:, cols], hn_all[:, cols])
+
+        def loads_after(n):
+            ci, r = divmod(n, 8)
+            if ci < LAST and r % 4 == 3:
+                done = 2 * ci + r // 4
+            elif ci == LAST and r % 2 == 1:
+                done = 2 * LAST + r // 2
+            else:
+                return
+            if done + WBUFS < NLOADS:
+                load(done + WBUFS)
+
+        NMAIN = 8 * LAST
+        xg = None
+        hgs = None
+        for n in range(NMAIN):
+            unit_t(n, "V" if n % 16 in V_COPIES else "S")
+            loads_after(n)
+            if n == 2:
+                xg = prepare_x()
+            if n == 4:
+                quantise(xg, act_codes[0][:], act_scales[0][:])
+            if n == 8:
+                hgs = prepare_h()
+            if n == 10:
+                for gp in range(2):
+                    cols = slice(gp * 256, (gp + 1) * 256)
+                    quantise(hgs[gp], act_codes[1][:, cols], act_scales[1][:, cols])
+            if n == 16:
+                prepare_ig()
+            if n in BIAS_AT:
+                spread_bias(BIAS_AT.index(n) % 2, BIAS_AT.index(n) // 2)
+            if n >= QLAG:
+                unit_q(n - QLAG)
+            m = n - MXLAG
+            if m >= 0 and m % 8 == 7:
+                chunk_mx(m // 8)
+                schedule_epilogue(n, m // 8)
+            for fn in deferred.get(n, []):
                 fn()
+
+        def block_t(j):
+            for s in range(2):
+                unit_t(NMAIN + 2 * j + s, "SS"[s])
+                loads_after(NMAIN + 2 * j + s)
+
+        def late(n):
+            for fn in deferred.get(n, []):
+                fn()
+
+        block_t(0)
+        unit_q(NMAIN - 2)
+        unit_q(NMAIN - 1)
+        late(NMAIN)
+        late(NMAIN + 1)
+        block_t(1)
+        unit_q(NMAIN)
+        unit_q(NMAIN + 1)
+        late(NMAIN + 2)
+        late(NMAIN + 3)
+        chunk_mx(LAST - 1)
+        block_t(2)
+        unit_q(NMAIN + 2)
+        unit_q(NMAIN + 3)
+        late(NMAIN + 4)
+        late(NMAIN + 5)
+        ep_z(3, 1)
+        keep_zpart()
+        block_t(3)
+        unit_q(NMAIN + 4)
+        unit_q(NMAIN + 5)
+        for j in range(3):
+            block_mx(j)
+        unit_q(NMAIN + 6)
+        unit_q(NMAIN + 7)
+        block_mx(3)
+        for j in range(3):
+            last_z(j)
+            last_sig(j)
+        for j in range(3):
+            last_h(j)
+        last_z(3)
+        last_sig(3)
+        last_h(3)

@@ -17,22 +17,23 @@ K = 2048
 HID = 2048
 NCOL = 512
 WBUFS = 10
-QLAG = 2
-MXLAG = 6
-V_COPIES = (3, 8, 13)
-EARLY_STORES = 0
-BIAS_AT = (9, 10, 11, 12, 13, 14, 15, 17)
+V_BANKS = (1, 5)
+V_BANKS_EARLY = (1, 3, 5)
+EARLY_UNITS = 8
+BIAS_AT = (2, 2, 3, 3, 4, 4, 5, 5)
+SMALL_LOADS = (("x", 2), ("h", 3), ("ig", 4), ("c", 4))
+X_AT = 1
+H_AT = 2
+IG_AT = 4
+C_AT = 0
+TAIL_FROM = 30
 
 FLOPS = 2 * 4 * 2048 * 2048 * 128
 
-CHUNKS = (
-    (0, 0), (1, 0), (2, 0), (3, 0),
-    (0, 1), (1, 1), (2, 1), (3, 1),
-    (0, 2), (1, 2), (0, 3), (1, 3),
-    (2, 2), (3, 2), (2, 3), (3, 3),
-)
-NCH = len(CHUNKS)
-LAST = NCH - 1
+GATE_ORDER = ((0, 0), (1, 0), (0, 1), (1, 1), (0, 2), (0, 3), (1, 2), (1, 3))
+LAST_GATE = (1, 3)
+END_BACK = 3
+ACC_BANK = {(0, 0): 0, (1, 0): 1, (0, 1): 0, (1, 1): 1, (0, 2): 0, (0, 3): 1, (1, 2): 0, (1, 3): 1}
 
 
 def tile_naivelstm_pb_kernel(
@@ -43,16 +44,13 @@ def tile_naivelstm_pb_kernel(
         ctx.enter_context(tc.manual_schedule())
         const = ctx.enter_context(tc.tile_pool(name="const", bufs=1))
         wpool = ctx.enter_context(tc.tile_pool(name="wpool", bufs=WBUFS))
-        gpool = ctx.enter_context(tc.tile_pool(name="gpool", bufs=8))
-        cpool = ctx.enter_context(tc.tile_pool(name="cpool", bufs=3))
+        gpool = ctx.enter_context(tc.tile_pool(name="gpool", bufs=3))
+        cpool = ctx.enter_context(tc.tile_pool(name="cpool", bufs=6))
         ep = ctx.enter_context(tc.tile_pool(name="ep", bufs=2))
         accp = ctx.enter_context(tc.psum_pool(name="accp", bufs=1))
         tp = ctx.enter_context(tc.psum_pool(name="tp", bufs=6))
 
-        w_views = [
-            w.rearrange("(a q s r) k -> a s q (r k)", a=4, q=P, s=2, r=2)
-            for w in (w_if, w_hf, w_io, w_ho)
-        ]
+        weights = (w_if, w_hf, w_io, w_ho)
 
         ident32 = const.tile([P, P], F32, name="ident32")
         identb = const.tile([P, P], BF16, name="identb")
@@ -66,28 +64,47 @@ def tile_naivelstm_pb_kernel(
         nc.vector.memset(warm[:], 0.0)
         nc.scalar.activation(out=warm[:, 1:2], in_=warm[:, 0:1], func=ACT.Sigmoid)
 
-        NLOADS = 2 * LAST + 4
+        units = []
+        for gate, a in GATE_ORDER:
+            for jp in range(2):
+                for opnd in range(2):
+                    if (gate, a, jp, opnd) == (1, 3, 1, 1):
+                        for r in range(2):
+                            units.append(("block", 2 * gate + opnd, a, jp, r))
+                    else:
+                        units.append(("half", 2 * gate + opnd, a, jp, 0))
+        NUNITS = len(units)
+        NMAIN = NUNITS - 2
+
         wt = {}
-        stores = {"open": False, "early": EARLY_STORES, "pending": []}
+        stores = {"open": False, "pending": []}
 
         def load(n):
-            if n < 2 * LAST:
-                t = wpool.tile([P, 2 * K], BF16, name="wt", tag="wt")
-                wsel, a = CHUNKS[n // 2]
-                nc.sync.dma_start(out=t[:], in_=w_views[wsel][a, n % 2, :, :])
-            else:
-                j = n - 2 * LAST
+            kind, wsel, a, jp, r = units[n]
+            w = weights[wsel]
+            if kind == "block":
                 t = wpool.tile([P, K], BF16, name="wt", tag="wt")
-                nc.sync.dma_start(out=t[:], in_=w_ho[3 * NCOL + j * P : 3 * NCOL + (j + 1) * P, :])
+                nc.sync.dma_start(
+                    out=t[:], in_=w.rearrange("(a s r q) k -> a s r q k", a=4, s=2, r=2, q=P)[a, jp, r, :, :]
+                )
+            elif (wsel // 2, a) == LAST_GATE:
+                t = wpool.tile([P, 2, K], BF16, name="wt", tag="wt")
+                nc.sync.dma_start(
+                    out=t[:], in_=w.rearrange("(a s r q) k -> a s q r k", a=4, s=2, r=2, q=P)[a, jp, :, :, :]
+                )
+            else:
+                t = wpool.tile([P, 2, K], BF16, name="wt", tag="wt")
+                nc.sync.dma_start(
+                    out=t[:], in_=w.rearrange("(a q s r) k -> a s q r k", a=4, q=P, s=2, r=2)[a, jp, :, :, :]
+                )
             wt[n] = t
-            if n == NLOADS - 1:
+            if n == NUNITS - 1:
                 stores["open"] = True
                 for dst, src in stores["pending"]:
                     nc.sync.dma_start(out=dst, in_=src)
 
         def store(dst, src):
-            if stores["open"] or stores["early"] > 0:
-                stores["early"] = stores["early"] - 1
+            if stores["open"]:
                 nc.sync.dma_start(out=dst, in_=src)
             else:
                 stores["pending"].append((dst, src))
@@ -101,17 +118,31 @@ def tile_naivelstm_pb_kernel(
                 out=brow[row : row + 1, gate * HID : (gate + 1) * HID],
                 in_=b.rearrange("n o -> o n"),
             )
-        load(0)
-        nc.sync.dma_start(out=xraw[:], in_=x.rearrange("(s p e) b -> p s e b", s=8, p=P, e=2))
-        load(1)
-        nc.sync.dma_start(out=h_sb[:], in_=h)
-        load(2)
-        load(3)
-        nc.sync.dma_start(out=ig_sb[:], in_=ig.rearrange("(a q j) b -> q a (j b)", a=4, q=P, j=4))
-        load(4)
-        nc.sync.dma_start(out=c_sb[:], in_=c)
-        for n in range(5, WBUFS):
-            load(n)
+        progress = {"loaded": 0, "freed": 0}
+
+        def small_load(what):
+            if what == "x":
+                nc.sync.dma_start(out=xraw[:], in_=x.rearrange("(s p e) b -> p s e b", s=8, p=P, e=2))
+            elif what == "h":
+                nc.sync.dma_start(out=h_sb[:], in_=h)
+            elif what == "ig":
+                nc.sync.dma_start(out=ig_sb[:], in_=ig.rearrange("(a q j) b -> q a (j b)", a=4, q=P, j=4))
+            else:
+                nc.sync.dma_start(out=c_sb[:], in_=c)
+
+        def next_loads():
+            while progress["loaded"] < NUNITS and progress["loaded"] - progress["freed"] < WBUFS:
+                for what, before in SMALL_LOADS:
+                    if before == progress["loaded"]:
+                        small_load(what)
+                load(progress["loaded"])
+                progress["loaded"] = progress["loaded"] + 1
+
+        next_loads()
+
+        def loads_after(k):
+            progress["freed"] = progress["freed"] + 1
+            next_loads()
 
         def transpose_bank(src32, cols):
             bank = tp.tile([P, 2, 2, P], F32, name="xt", tag="xt")
@@ -121,18 +152,14 @@ def tile_naivelstm_pb_kernel(
                     nc.tensor.transpose(bank[:, u, s, :], src32[:, col : col + P], ident32[:])
             return bank
 
-        def copy_bank(eng, bank):
-            grouped = gpool.tile([P, K // 2], BF16, name="grouped", tag="grouped", align_bytes=64)
+        def copy_bank(eng, grouped, slot, bank):
             dst = grouped[:].bitcast(F32).rearrange("p (n u) -> p n u", u=2)
+            dst = dst[:, slot * 256 : (slot + 1) * 256, :]
             src = bank[:].rearrange("p u s q -> p (s q) u")
             if eng == "S":
                 nc.scalar.copy(out=dst, in_=src)
             else:
                 nc.vector.tensor_copy(out=dst, in_=src)
-            return grouped
-
-        def quantise(grouped, codes, scales):
-            nc.vector.quantize_mx(out=codes.bitcast(FP8X4), scales=scales, in_=grouped[:])
 
         def row_block_cols(gp):
             return [[(2 * (2 * gp + s) + u) * P for s in range(2)] for u in range(2)]
@@ -142,19 +169,28 @@ def tile_naivelstm_pb_kernel(
         for nm in ("x", "h"):
             act_codes.append(const.tile([P, 512], U32, name="codes_" + nm, align_bytes=64))
             act_scales.append(const.tile([P, 512], U8, name="scales_" + nm, align_bytes=64))
+        act_grouped = {}
 
         def prepare_x():
-            xg = const.tile([P, K], BF16, name="xg", align_bytes=64)
+            xg = gpool.tile([P, K], BF16, name="grouped", tag="grouped", align_bytes=64)
             nc.vector.tensor_copy(
                 out=xg[:].rearrange("p (g b t) -> p g b t", g=4, b=P, t=4),
                 in_=xraw[:].rearrange("p (g u) e b -> p g b (u e)", g=4, u=2),
             )
-            return xg
+            act_grouped[0] = xg
 
         def prepare_h():
             h32 = h_sb[:].bitcast(F32)
+            hg = gpool.tile([P, K], BF16, name="grouped", tag="grouped", align_bytes=64)
             hbanks = [transpose_bank(h32, row_block_cols(gp)) for gp in range(2)]
-            return [copy_bank("SV"[gp], hbanks[gp]) for gp in range(2)]
+            for gp in range(2):
+                copy_bank("SV"[gp], hg, gp, hbanks[gp])
+            act_grouped[1] = hg
+
+        def quantise_act(opnd):
+            nc.vector.quantize_mx(
+                out=act_codes[opnd][:].bitcast(FP8X4), scales=act_scales[opnd][:], in_=act_grouped[opnd][:]
+            )
 
         igT = const.tile([P, 4, 4, P], BF16, name="igT")
 
@@ -188,60 +224,74 @@ def tile_naivelstm_pb_kernel(
         th = {}
         blk = {}
         deferred = {}
+        banks_done = {"n": 0}
 
         def defer(slot, fn):
             deferred[slot] = deferred.get(slot, []) + [fn]
 
-        def unit_t(n, eng):
-            ci, r = divmod(n, 8)
-            first, second = divmod(r, 4) if ci < LAST else divmod(r, 2)
-            if ci < LAST:
-                w32 = wt[2 * ci + first][:].bitcast(F32)
-                cols = [[s * 1024 + (2 * second + u) * P for s in range(2)] for u in range(2)]
-            else:
-                w32 = wt[2 * LAST + first][:].bitcast(F32)
-                cols = row_block_cols(second)
-            grouped[n] = copy_bank(eng, transpose_bank(w32, cols))
+        def late(slot):
+            for fn in deferred.get(slot, []):
+                fn()
 
-        def unit_q(n):
-            ci, r = divmod(n, 8)
-            if r == 0:
-                codes[ci] = cpool.tile([P, 4, NCOL], U32, name="codes", tag="codes", align_bytes=64)
-                scales[ci] = cpool.tile([P, 4, NCOL], U8, name="scales", tag="scales", align_bytes=64)
-            if ci < LAST:
-                half, row = divmod(r, 4)
+        def unit_t(k, engines=None):
+            kind = units[k][0]
+            w32 = wt[k][:]
+            if kind == "half":
+                w32 = w32.rearrange("p r k -> p (r k)")
+            w32 = w32.bitcast(F32)
+            if kind == "block":
+                grouped[k] = gpool.tile([P, K], BF16, name="grouped", tag="grouped", align_bytes=64)
+                colmaps = [row_block_cols(gp) for gp in range(2)]
             else:
-                row, half = divmod(r, 2)
-            cols = slice(half * 256, (half + 1) * 256)
-            quantise(grouped[n], codes[ci][:, row, cols], scales[ci][:, row, cols])
+                grouped[k] = gpool.tile([P, 2 * K], BF16, name="grouped", tag="grouped", align_bytes=64)
+                colmaps = [[[s * 1024 + (2 * g + u) * P for s in range(2)] for u in range(2)] for g in range(4)]
+            for slot in range(len(colmaps)):
+                bank = transpose_bank(w32, colmaps[slot])
+                if engines is None and k >= TAIL_FROM:
+                    eng = "S"
+                elif engines is None:
+                    eng = "V" if (banks_done["n"] % 8 in V_BANKS_EARLY if k < EARLY_UNITS else banks_done["n"] % 16 in (1, 6, 11)) else "S"
+                else:
+                    eng = engines[slot]
+                banks_done["n"] = banks_done["n"] + 1
+                copy_bank(eng, grouped[k], slot, bank)
 
-        def mx(out, opnd, g, ci, row, cols, start, stop):
+        def unit_q(k):
+            width = NCOL if units[k][0] == "block" else 2 * NCOL
+            codes[k] = cpool.tile([P, width], U32, name="codes", tag="codes", align_bytes=64)
+            scales[k] = cpool.tile([P, width], U8, name="scales", tag="scales", align_bytes=64)
+            nc.vector.quantize_mx(
+                out=codes[k][:].bitcast(FP8X4), scales=scales[k][:], in_=grouped[k][:]
+            )
+
+        def mx(out, opnd, g, k, cols, start, stop):
             nc.tensor.matmul_mx(
                 out=out,
                 lhsT=act_codes[opnd][:, g * P : (g + 1) * P].bitcast(FP8X4),
                 lhsT_scale=act_scales[opnd][:, g * P : (g + 1) * P],
-                rhs=codes[ci][:, row, cols].bitcast(FP8X4),
-                rhs_scale=scales[ci][:, row, cols],
+                rhs=codes[k][:, cols].bitcast(FP8X4),
+                rhs_scale=scales[k][:, cols],
                 start=start,
                 stop=stop,
             )
 
-        def chunk_mx(ci):
-            wsel, a = CHUNKS[ci]
+        def unit_mx(k):
+            kind, wsel, a, jp, r = units[k]
             gate, opnd = divmod(wsel, 2)
-            alone = (wsel, a) == (2, 3)
-            if opnd == 0:
-                acc[gate] = accp.tile([P, NCOL], F32, name="acc%d" % gate, tag="acc%d" % gate)
-            for g in range(4):
-                mx(acc[gate][:], opnd, g, ci, g, slice(0, NCOL), opnd == 0 and g == 0, (opnd == 1 or alone) and g == 3)
-
-        def block_mx(j):
-            if j < 2:
-                blk[j] = accp.tile([P, P], F32, name="acc%d" % j, tag="acc%d" % j)
+            if kind == "half":
+                alone = (gate, a, jp) == (1, 3, 1)
+                if opnd == 0 and jp == 0:
+                    bank = ACC_BANK[(gate, a)]
+                    acc[gate] = accp.tile([P, NCOL], F32, name="acc%d" % bank, tag="acc%d" % bank)
+                for g in range(4):
+                    mx(
+                        acc[gate][:, jp * 256 : (jp + 1) * 256], opnd, g, k, slice(g * 256, (g + 1) * 256),
+                        opnd == 0 and g == 0, (opnd == 1 or alone) and g == 3,
+                    )
             else:
-                blk[j] = tp.tile([P, P], F32, name="blk", tag="xt")
-            for g in range(4):
-                mx(blk[j][:], 1, g, LAST, j, slice(g * P, (g + 1) * P), g == 0, g == 3)
+                blk[r] = tp.tile([P, P], F32, name="blk", tag="xt")
+                for g in range(4):
+                    mx(blk[r][:], 1, g, k, slice(g * P, (g + 1) * P), g == 0, g == 3)
 
         def natural(ap):
             return ap.rearrange("p (q j) -> p q j", j=4)
@@ -256,15 +306,15 @@ def tile_naivelstm_pb_kernel(
             )
             state["z"] = z
 
-        def ep_sig():
-            s = ep.tile([P, NCOL], F32, name="sg", tag="sg")
+        def ep_sig(a, gate):
+            s = ep.tile([P, NCOL], F32, name="sg", tag="sg", bufs=4)
             nc.scalar.activation(out=s[:], in_=state["z"][:], func=ACT.Sigmoid)
-            state["s"] = s
+            state[(gate, a)] = s
 
         def ep_cnext(a):
             cols = slice(a * NCOL, (a + 1) * NCOL)
             t = ep.tile([P, NCOL], F32, name="fc", tag="fc")
-            nc.vector.tensor_tensor(out=t[:], in0=state["s"][:], in1=c_sb[:, cols], op=ALU.mult)
+            nc.vector.tensor_tensor(out=t[:], in0=state[(0, a)][:], in1=c_sb[:, cols], op=ALU.mult)
             nc.vector.tensor_tensor(
                 out=natural(cn_all[:, cols]),
                 in0=natural(t[:]),
@@ -280,126 +330,78 @@ def tile_naivelstm_pb_kernel(
 
         def ep_hnext(a):
             cols = slice(a * NCOL, (a + 1) * NCOL)
-            nc.vector.tensor_tensor(out=hn_all[:, cols], in0=state["s"][:], in1=th[a][:], op=ALU.mult)
+            nc.vector.tensor_tensor(out=hn_all[:, cols], in0=state[(1, a)][:], in1=th[a][:], op=ALU.mult)
             store(out_0[:, cols], hn_all[:, cols])
 
-        def keep_zpart():
-            state["zpart"] = state["z"]
-
-        def schedule_epilogue(slot, ci):
-            wsel, a = CHUNKS[ci]
-            if wsel == 1:
+        def schedule_epilogue(slot, k):
+            kind, wsel, a, jp, r = units[k]
+            if jp == 1 and wsel == 1:
                 defer(slot + 1, lambda: ep_z(a, 0))
-                defer(slot + 3, ep_sig)
-                defer(slot + 5, lambda: ep_cnext(a))
-                defer(slot + 7, lambda: ep_tanh(a))
-            if wsel == 3:
+                defer(slot + 2, lambda: ep_sig(a, 0))
+                defer(max(slot + 3, C_AT), lambda: ep_cnext(a))
+                defer(max(slot + 4, C_AT + 1), lambda: ep_tanh(a))
+            if jp == 1 and wsel == 3:
                 defer(slot + 1, lambda: ep_z(a, 1))
-                defer(slot + 3, ep_sig)
-                defer(slot + 5, lambda: ep_hnext(a))
-            if (wsel, a) == (2, 3):
-                defer(slot + 1, lambda: ep_z(a, 1))
-                defer(slot + 1, keep_zpart)
+                defer(slot + 2, lambda: ep_sig(a, 1))
+                defer(max(slot + 3, C_AT + 2), lambda: ep_hnext(a))
 
-        def last_z(j):
-            zl = ep.tile([P, P], F32, name="zl", tag="zl", bufs=4)
+        zlast = const.tile([P, NCOL], F32, name="zlast")
+        slast = const.tile([P, NCOL], F32, name="slast")
+
+        def last_zpart():
             nc.vector.tensor_tensor(
-                out=zl[:], in0=blk[j][:], in1=state["zpart"][:, j * P : (j + 1) * P], op=ALU.add
+                out=zlast[:], in0=acc[1][:], in1=bias[:, HID + 3 * NCOL : HID + 4 * NCOL], op=ALU.add
             )
-            state["zl%d" % j] = zl
 
-        def last_sig(j):
-            sl = ep.tile([P, P], F32, name="sl", tag="sl", bufs=4)
-            nc.scalar.activation(out=sl[:], in_=state["zl%d" % j][:], func=ACT.Sigmoid)
-            state["sl%d" % j] = sl
-
-        def last_h(j):
-            cols = slice(3 * NCOL + j * P, 3 * NCOL + (j + 1) * P)
-            nc.vector.tensor_tensor(
-                out=hn_all[:, cols], in0=state["sl%d" % j][:], in1=th[3][:, j * P : (j + 1) * P], op=ALU.mult
-            )
+        def last_out(lo, hi):
+            nc.scalar.activation(out=slast[:, lo:hi], in_=zlast[:, lo:hi], func=ACT.Sigmoid)
+            cols = slice(3 * NCOL + lo, 3 * NCOL + hi)
+            nc.vector.tensor_tensor(out=hn_all[:, cols], in0=slast[:, lo:hi], in1=th[3][:, lo:hi], op=ALU.mult)
             store(out_0[:, cols], hn_all[:, cols])
 
-        def loads_after(n):
-            ci, r = divmod(n, 8)
-            if ci < LAST and r % 4 == 3:
-                done = 2 * ci + r // 4
-            elif ci == LAST and r % 2 == 1:
-                done = 2 * LAST + r // 2
-            else:
-                return
-            if done + WBUFS < NLOADS:
-                load(done + WBUFS)
+        def last_z(r):
+            cols = slice((2 + r) * P, (3 + r) * P)
+            nc.vector.tensor_tensor(out=zlast[:, cols], in0=blk[r][:], in1=zlast[:, cols], op=ALU.add)
 
-        NMAIN = 8 * LAST
-        xg = None
-        hgs = None
-        for n in range(NMAIN):
-            unit_t(n, "V" if n % 16 in V_COPIES else "S")
-            loads_after(n)
-            if n == 2:
-                xg = prepare_x()
-            if n == 4:
-                quantise(xg, act_codes[0][:], act_scales[0][:])
-            if n == 8:
-                hgs = prepare_h()
-            if n == 10:
-                for gp in range(2):
-                    cols = slice(gp * 256, (gp + 1) * 256)
-                    quantise(hgs[gp], act_codes[1][:, cols], act_scales[1][:, cols])
-            if n == 16:
+        for k in range(NMAIN):
+            unit_t(k)
+            loads_after(k)
+            if k >= 1:
+                unit_q(k - 1)
+            if k == X_AT:
+                prepare_x()
+            if k == H_AT:
+                prepare_h()
+            if k == X_AT + 1:
+                quantise_act(0)
+            if k == H_AT + 1:
+                quantise_act(1)
+            if k == IG_AT:
                 prepare_ig()
-            if n in BIAS_AT:
-                spread_bias(BIAS_AT.index(n) % 2, BIAS_AT.index(n) // 2)
-            if n >= QLAG:
-                unit_q(n - QLAG)
-            m = n - MXLAG
-            if m >= 0 and m % 8 == 7:
-                chunk_mx(m // 8)
-                schedule_epilogue(n, m // 8)
-            for fn in deferred.get(n, []):
-                fn()
+            for n in range(8):
+                if BIAS_AT[n] == k:
+                    spread_bias(n % 2, n // 2)
+            if k % 2 == 1 and k >= 3:
+                for m in (k - 3, k - 2):
+                    unit_mx(m)
+                    schedule_epilogue(k, m)
+            late(k)
 
-        def block_t(j):
-            for s in range(2):
-                unit_t(NMAIN + 2 * j + s, "SS"[s])
-                loads_after(NMAIN + 2 * j + s)
-
-        def late(n):
-            for fn in deferred.get(n, []):
-                fn()
-
-        block_t(0)
-        unit_q(NMAIN - 2)
+        unit_t(NMAIN, "SS")
         unit_q(NMAIN - 1)
         late(NMAIN)
-        late(NMAIN + 1)
-        block_t(1)
+        unit_t(NMAIN + 1, "SS")
+        for m in range(NMAIN - END_BACK, NMAIN):
+            unit_mx(m)
         unit_q(NMAIN)
+        unit_mx(NMAIN)
+        last_zpart()
         unit_q(NMAIN + 1)
+        unit_mx(NMAIN + 1)
+        last_z(0)
+        late(NMAIN + 1)
         late(NMAIN + 2)
         late(NMAIN + 3)
-        chunk_mx(LAST - 1)
-        block_t(2)
-        unit_q(NMAIN + 2)
-        unit_q(NMAIN + 3)
-        late(NMAIN + 4)
-        late(NMAIN + 5)
-        ep_z(3, 1)
-        keep_zpart()
-        block_t(3)
-        unit_q(NMAIN + 4)
-        unit_q(NMAIN + 5)
-        for j in range(3):
-            block_mx(j)
-        unit_q(NMAIN + 6)
-        unit_q(NMAIN + 7)
-        block_mx(3)
-        for j in range(3):
-            last_z(j)
-            last_sig(j)
-        for j in range(3):
-            last_h(j)
-        last_z(3)
-        last_sig(3)
-        last_h(3)
+        last_out(0, 384)
+        last_z(1)
+        last_out(384, 512)

@@ -17,23 +17,22 @@ K = 2048
 HID = 2048
 NCOL = 512
 WBUFS = 10
-V_BANKS = (1, 5)
-V_BANKS_EARLY = (1, 3, 5)
-EARLY_UNITS = 8
-BIAS_AT = (2, 2, 3, 3, 4, 4, 5, 5)
-SMALL_LOADS = (("x", 2), ("h", 3), ("ig", 4), ("c", 4))
-X_AT = 1
-H_AT = 2
-IG_AT = 4
-C_AT = 0
-TAIL_FROM = 30
+QLAG = 2
+MXLAG = 6
+V_COPIES = (3, 8, 13)
+EARLY_STORES = 0
+BIAS_AT = (9, 10, 11, 12, 13, 14, 15, 17)
 
 FLOPS = 2 * 4 * 2048 * 2048 * 128
 
-GATE_ORDER = ((0, 0), (1, 0), (0, 1), (1, 1), (0, 2), (0, 3), (1, 2), (1, 3))
-LAST_GATE = (1, 3)
-END_BACK = 3
-ACC_BANK = {(0, 0): 0, (1, 0): 1, (0, 1): 0, (1, 1): 1, (0, 2): 0, (0, 3): 1, (1, 2): 0, (1, 3): 1}
+CHUNKS = (
+    (0, 0), (1, 0), (2, 0), (3, 0),
+    (0, 1), (1, 1), (2, 1), (3, 1),
+    (0, 2), (1, 2), (0, 3), (1, 3),
+    (2, 2), (3, 2), (2, 3), (3, 3),
+)
+NCH = len(CHUNKS)
+LAST = NCH - 1
 
 
 def tile_naivelstm_pb_kernel(
@@ -44,13 +43,16 @@ def tile_naivelstm_pb_kernel(
         ctx.enter_context(tc.manual_schedule())
         const = ctx.enter_context(tc.tile_pool(name="const", bufs=1))
         wpool = ctx.enter_context(tc.tile_pool(name="wpool", bufs=WBUFS))
-        gpool = ctx.enter_context(tc.tile_pool(name="gpool", bufs=3))
-        cpool = ctx.enter_context(tc.tile_pool(name="cpool", bufs=6))
+        gpool = ctx.enter_context(tc.tile_pool(name="gpool", bufs=8))
+        cpool = ctx.enter_context(tc.tile_pool(name="cpool", bufs=3))
         ep = ctx.enter_context(tc.tile_pool(name="ep", bufs=2))
         accp = ctx.enter_context(tc.psum_pool(name="accp", bufs=1))
         tp = ctx.enter_context(tc.psum_pool(name="tp", bufs=6))
 
-        weights = (w_if, w_hf, w_io, w_ho)
+        w_views = [
+            w.rearrange("(a q s r) k -> a s q (r k)", a=4, q=P, s=2, r=2)
+            for w in (w_if, w_hf, w_io, w_ho)
+        ]
 
         ident32 = const.tile([P, P], F32, name="ident32")
         identb = const.tile([P, P], BF16, name="identb")
@@ -64,47 +66,28 @@ def tile_naivelstm_pb_kernel(
         nc.vector.memset(warm[:], 0.0)
         nc.scalar.activation(out=warm[:, 1:2], in_=warm[:, 0:1], func=ACT.Sigmoid)
 
-        units = []
-        for gate, a in GATE_ORDER:
-            for jp in range(2):
-                for opnd in range(2):
-                    if (gate, a, jp, opnd) == (1, 3, 1, 1):
-                        for r in range(2):
-                            units.append(("block", 2 * gate + opnd, a, jp, r))
-                    else:
-                        units.append(("half", 2 * gate + opnd, a, jp, 0))
-        NUNITS = len(units)
-        NMAIN = NUNITS - 2
-
+        NLOADS = 2 * LAST + 4
         wt = {}
-        stores = {"open": False, "pending": []}
+        stores = {"open": False, "early": EARLY_STORES, "pending": []}
 
         def load(n):
-            kind, wsel, a, jp, r = units[n]
-            w = weights[wsel]
-            if kind == "block":
-                t = wpool.tile([P, K], BF16, name="wt", tag="wt")
-                nc.sync.dma_start(
-                    out=t[:], in_=w.rearrange("(a s r q) k -> a s r q k", a=4, s=2, r=2, q=P)[a, jp, r, :, :]
-                )
-            elif (wsel // 2, a) == LAST_GATE:
-                t = wpool.tile([P, 2, K], BF16, name="wt", tag="wt")
-                nc.sync.dma_start(
-                    out=t[:], in_=w.rearrange("(a s r q) k -> a s q r k", a=4, s=2, r=2, q=P)[a, jp, :, :, :]
-                )
+            if n < 2 * LAST:
+                t = wpool.tile([P, 2 * K], BF16, name="wt", tag="wt")
+                wsel, a = CHUNKS[n // 2]
+                nc.sync.dma_start(out=t[:], in_=w_views[wsel][a, n % 2, :, :])
             else:
-                t = wpool.tile([P, 2, K], BF16, name="wt", tag="wt")
-                nc.sync.dma_start(
-                    out=t[:], in_=w.rearrange("(a q s r) k -> a s q r k", a=4, q=P, s=2, r=2)[a, jp, :, :, :]
-                )
+                j = n - 2 * LAST
+                t = wpool.tile([P, K], BF16, name="wt", tag="wt")
+                nc.sync.dma_start(out=t[:], in_=w_ho[3 * NCOL + j * P : 3 * NCOL + (j + 1) * P, :])
             wt[n] = t
-            if n == NUNITS - 1:
+            if n == NLOADS - 1:
                 stores["open"] = True
                 for dst, src in stores["pending"]:
                     nc.sync.dma_start(out=dst, in_=src)
 
         def store(dst, src):
-            if stores["open"]:
+            if stores["open"] or stores["early"] > 0:
+                stores["early"] = stores["early"] - 1
                 nc.sync.dma_start(out=dst, in_=src)
             else:
                 stores["pending"].append((dst, src))
@@ -118,31 +101,17 @@ def tile_naivelstm_pb_kernel(
                 out=brow[row : row + 1, gate * HID : (gate + 1) * HID],
                 in_=b.rearrange("n o -> o n"),
             )
-        progress = {"loaded": 0, "freed": 0}
-
-        def small_load(what):
-            if what == "x":
-                nc.sync.dma_start(out=xraw[:], in_=x.rearrange("(s p e) b -> p s e b", s=8, p=P, e=2))
-            elif what == "h":
-                nc.sync.dma_start(out=h_sb[:], in_=h)
-            elif what == "ig":
-                nc.sync.dma_start(out=ig_sb[:], in_=ig.rearrange("(a q j) b -> q a (j b)", a=4, q=P, j=4))
-            else:
-                nc.sync.dma_start(out=c_sb[:], in_=c)
-
-        def next_loads():
-            while progress["loaded"] < NUNITS and progress["loaded"] - progress["freed"] < WBUFS:
-                for what, before in SMALL_LOADS:
-                    if before == progress["loaded"]:
-                        small_load(what)
-                load(progress["loaded"])
-                progress["loaded"] = progress["loaded"] + 1
-
-        next_loads()
-
-        def loads_after(k):
-            progress["freed"] = progress["freed"] + 1
-            next_loads()
+        load(0)
+        nc.sync.dma_start(out=xraw[:], in_=x.rearrange("(s p e) b -> p s e b", s=8, p=P, e=2))
+        load(1)
+        nc.sync.dma_start(out=h_sb[:], in_=h)
+        load(2)
+        load(3)
+        nc.sync.dma_start(out=ig_sb[:], in_=ig.rearrange("(a q j) b -> q a (j b)", a=4, q=P, j=4))
+        load(4)
+        nc.sync.dma_start(out=c_sb[:], in_=c)
+        for n in range(5, WBUFS):
+            load(n)
 
         def transpose_bank(src32, cols):
             bank = tp.tile([P, 2, 2, P], F32, name="xt", tag="xt")
@@ -152,14 +121,18 @@ def tile_naivelstm_pb_kernel(
                     nc.tensor.transpose(bank[:, u, s, :], src32[:, col : col + P], ident32[:])
             return bank
 
-        def copy_bank(eng, grouped, slot, bank):
+        def copy_bank(eng, bank):
+            grouped = gpool.tile([P, K // 2], BF16, name="grouped", tag="grouped", align_bytes=64)
             dst = grouped[:].bitcast(F32).rearrange("p (n u) -> p n u", u=2)
-            dst = dst[:, slot * 256 : (slot + 1) * 256, :]
             src = bank[:].rearrange("p u s q -> p (s q) u")
             if eng == "S":
                 nc.scalar.copy(out=dst, in_=src)
             else:
                 nc.vector.tensor_copy(out=dst, in_=src)
+            return grouped
+
+        def quantise(grouped, codes, scales):
+            nc.vector.quantize_mx(out=codes.bitcast(FP8X4), scales=scales, in_=grouped[:])
 
         def row_block_cols(gp):
             return [[(2 * (2 * gp + s) + u) * P for s in range(2)] for u in range(2)]
@@ -169,28 +142,19 @@ def tile_naivelstm_pb_kernel(
         for nm in ("x", "h"):
             act_codes.append(const.tile([P, 512], U32, name="codes_" + nm, align_bytes=64))
             act_scales.append(const.tile([P, 512], U8, name="scales_" + nm, align_bytes=64))
-        act_grouped = {}
 
         def prepare_x():
-            xg = gpool.tile([P, K], BF16, name="grouped", tag="grouped", align_bytes=64)
+            xg = const.tile([P, K], BF16, name="xg", align_bytes=64)
             nc.vector.tensor_copy(
                 out=xg[:].rearrange("p (g b t) -> p g b t", g=4, b=P, t=4),
                 in_=xraw[:].rearrange("p (g u) e b -> p g b (u e)", g=4, u=2),
             )
-            act_grouped[0] = xg
+            return xg
 
         def prepare_h():
             h32 = h_sb[:].bitcast(F32)
-            hg = gpool.tile([P, K], BF16, name="grouped", tag="grouped", align_bytes=64)
             hbanks = [transpose_bank(h32, row_block_cols(gp)) for gp in range(2)]
-            for gp in range(2):
-                copy_bank("SV"[gp], hg, gp, hbanks[gp])
-            act_grouped[1] = hg
-
-        def quantise_act(opnd):
-            nc.vector.quantize_mx(
-                out=act_codes[opnd][:].bitcast(FP8X4), scales=act_scales[opnd][:], in_=act_grouped[opnd][:]
-            )
+            return [copy_bank("SV"[gp], hbanks[gp]) for gp in range(2)]
 
         igT = const.tile([P, 4, 4, P], BF16, name="igT")
 
@@ -224,74 +188,60 @@ def tile_naivelstm_pb_kernel(
         th = {}
         blk = {}
         deferred = {}
-        banks_done = {"n": 0}
 
         def defer(slot, fn):
             deferred[slot] = deferred.get(slot, []) + [fn]
 
-        def late(slot):
-            for fn in deferred.get(slot, []):
-                fn()
-
-        def unit_t(k, engines=None):
-            kind = units[k][0]
-            w32 = wt[k][:]
-            if kind == "half":
-                w32 = w32.rearrange("p r k -> p (r k)")
-            w32 = w32.bitcast(F32)
-            if kind == "block":
-                grouped[k] = gpool.tile([P, K], BF16, name="grouped", tag="grouped", align_bytes=64)
-                colmaps = [row_block_cols(gp) for gp in range(2)]
+        def unit_t(n, eng):
+            ci, r = divmod(n, 8)
+            first, second = divmod(r, 4) if ci < LAST else divmod(r, 2)
+            if ci < LAST:
+                w32 = wt[2 * ci + first][:].bitcast(F32)
+                cols = [[s * 1024 + (2 * second + u) * P for s in range(2)] for u in range(2)]
             else:
-                grouped[k] = gpool.tile([P, 2 * K], BF16, name="grouped", tag="grouped", align_bytes=64)
-                colmaps = [[[s * 1024 + (2 * g + u) * P for s in range(2)] for u in range(2)] for g in range(4)]
-            for slot in range(len(colmaps)):
-                bank = transpose_bank(w32, colmaps[slot])
-                if engines is None and k >= TAIL_FROM:
-                    eng = "S"
-                elif engines is None:
-                    eng = "V" if (banks_done["n"] % 8 in V_BANKS_EARLY if k < EARLY_UNITS else banks_done["n"] % 16 in (1, 6, 11)) else "S"
-                else:
-                    eng = engines[slot]
-                banks_done["n"] = banks_done["n"] + 1
-                copy_bank(eng, grouped[k], slot, bank)
+                w32 = wt[2 * LAST + first][:].bitcast(F32)
+                cols = row_block_cols(second)
+            grouped[n] = copy_bank(eng, transpose_bank(w32, cols))
 
-        def unit_q(k):
-            width = NCOL if units[k][0] == "block" else 2 * NCOL
-            codes[k] = cpool.tile([P, width], U32, name="codes", tag="codes", align_bytes=64)
-            scales[k] = cpool.tile([P, width], U8, name="scales", tag="scales", align_bytes=64)
-            nc.vector.quantize_mx(
-                out=codes[k][:].bitcast(FP8X4), scales=scales[k][:], in_=grouped[k][:]
-            )
+        def unit_q(n):
+            ci, r = divmod(n, 8)
+            if r == 0:
+                codes[ci] = cpool.tile([P, 4, NCOL], U32, name="codes", tag="codes", align_bytes=64)
+                scales[ci] = cpool.tile([P, 4, NCOL], U8, name="scales", tag="scales", align_bytes=64)
+            if ci < LAST:
+                half, row = divmod(r, 4)
+            else:
+                row, half = divmod(r, 2)
+            cols = slice(half * 256, (half + 1) * 256)
+            quantise(grouped[n], codes[ci][:, row, cols], scales[ci][:, row, cols])
 
-        def mx(out, opnd, g, k, cols, start, stop):
+        def mx(out, opnd, g, ci, row, cols, start, stop):
             nc.tensor.matmul_mx(
                 out=out,
                 lhsT=act_codes[opnd][:, g * P : (g + 1) * P].bitcast(FP8X4),
                 lhsT_scale=act_scales[opnd][:, g * P : (g + 1) * P],
-                rhs=codes[k][:, cols].bitcast(FP8X4),
-                rhs_scale=scales[k][:, cols],
+                rhs=codes[ci][:, row, cols].bitcast(FP8X4),
+                rhs_scale=scales[ci][:, row, cols],
                 start=start,
                 stop=stop,
             )
 
-        def unit_mx(k):
-            kind, wsel, a, jp, r = units[k]
+        def chunk_mx(ci, passes=(0, 1, 2, 3)):
+            wsel, a = CHUNKS[ci]
             gate, opnd = divmod(wsel, 2)
-            if kind == "half":
-                alone = (gate, a, jp) == (1, 3, 1)
-                if opnd == 0 and jp == 0:
-                    bank = ACC_BANK[(gate, a)]
-                    acc[gate] = accp.tile([P, NCOL], F32, name="acc%d" % bank, tag="acc%d" % bank)
-                for g in range(4):
-                    mx(
-                        acc[gate][:, jp * 256 : (jp + 1) * 256], opnd, g, k, slice(g * 256, (g + 1) * 256),
-                        opnd == 0 and g == 0, (opnd == 1 or alone) and g == 3,
-                    )
+            alone = (wsel, a) == (2, 3)
+            if opnd == 0 and passes[0] == 0:
+                acc[gate] = accp.tile([P, NCOL], F32, name="acc%d" % gate, tag="acc%d" % gate)
+            for g in passes:
+                mx(acc[gate][:], opnd, g, ci, g, slice(0, NCOL), opnd == 0 and g == 0, (opnd == 1 or alone) and g == 3)
+
+        def block_mx(j):
+            if j < 2:
+                blk[j] = accp.tile([P, P], F32, name="acc%d" % j, tag="acc%d" % j)
             else:
-                blk[r] = tp.tile([P, P], F32, name="blk", tag="xt")
-                for g in range(4):
-                    mx(blk[r][:], 1, g, k, slice(g * P, (g + 1) * P), g == 0, g == 3)
+                blk[j] = tp.tile([P, P], F32, name="blk", tag="xt")
+            for g in range(4):
+                mx(blk[j][:], 1, g, LAST, j, slice(g * P, (g + 1) * P), g == 0, g == 3)
 
         def natural(ap):
             return ap.rearrange("p (q j) -> p q j", j=4)
@@ -306,15 +256,15 @@ def tile_naivelstm_pb_kernel(
             )
             state["z"] = z
 
-        def ep_sig(a, gate):
-            s = ep.tile([P, NCOL], F32, name="sg", tag="sg", bufs=4)
+        def ep_sig():
+            s = ep.tile([P, NCOL], F32, name="sg", tag="sg")
             nc.scalar.activation(out=s[:], in_=state["z"][:], func=ACT.Sigmoid)
-            state[(gate, a)] = s
+            state["s"] = s
 
         def ep_cnext(a):
             cols = slice(a * NCOL, (a + 1) * NCOL)
             t = ep.tile([P, NCOL], F32, name="fc", tag="fc")
-            nc.vector.tensor_tensor(out=t[:], in0=state[(0, a)][:], in1=c_sb[:, cols], op=ALU.mult)
+            nc.vector.tensor_tensor(out=t[:], in0=state["s"][:], in1=c_sb[:, cols], op=ALU.mult)
             nc.vector.tensor_tensor(
                 out=natural(cn_all[:, cols]),
                 in0=natural(t[:]),
@@ -330,78 +280,132 @@ def tile_naivelstm_pb_kernel(
 
         def ep_hnext(a):
             cols = slice(a * NCOL, (a + 1) * NCOL)
-            nc.vector.tensor_tensor(out=hn_all[:, cols], in0=state[(1, a)][:], in1=th[a][:], op=ALU.mult)
+            nc.vector.tensor_tensor(out=hn_all[:, cols], in0=state["s"][:], in1=th[a][:], op=ALU.mult)
             store(out_0[:, cols], hn_all[:, cols])
 
-        def schedule_epilogue(slot, k):
-            kind, wsel, a, jp, r = units[k]
-            if jp == 1 and wsel == 1:
+        def keep_zpart():
+            state["zpart"] = state["z"]
+
+        def schedule_epilogue(slot, ci):
+            wsel, a = CHUNKS[ci]
+            if wsel == 1:
                 defer(slot + 1, lambda: ep_z(a, 0))
-                defer(slot + 2, lambda: ep_sig(a, 0))
-                defer(max(slot + 3, C_AT), lambda: ep_cnext(a))
-                defer(max(slot + 4, C_AT + 1), lambda: ep_tanh(a))
-            if jp == 1 and wsel == 3:
+                defer(slot + 3, ep_sig)
+                defer(slot + 5, lambda: ep_cnext(a))
+                defer(slot + 7, lambda: ep_tanh(a))
+            if wsel == 3:
                 defer(slot + 1, lambda: ep_z(a, 1))
-                defer(slot + 2, lambda: ep_sig(a, 1))
-                defer(max(slot + 3, C_AT + 2), lambda: ep_hnext(a))
+                defer(slot + 3, ep_sig)
+                defer(slot + 5, lambda: ep_hnext(a))
+            if (wsel, a) == (2, 3):
+                defer(slot + 1, lambda: ep_z(a, 1))
+                defer(slot + 1, keep_zpart)
 
-        zlast = const.tile([P, NCOL], F32, name="zlast")
-        slast = const.tile([P, NCOL], F32, name="slast")
-
-        def last_zpart():
+        def last_z(j):
+            zl = ep.tile([P, P], F32, name="zl", tag="zl", bufs=4)
             nc.vector.tensor_tensor(
-                out=zlast[:], in0=acc[1][:], in1=bias[:, HID + 3 * NCOL : HID + 4 * NCOL], op=ALU.add
+                out=zl[:], in0=blk[j][:], in1=state["zpart"][:, j * P : (j + 1) * P], op=ALU.add
             )
+            state["zl%d" % j] = zl
 
-        def last_out(lo, hi):
-            nc.scalar.activation(out=slast[:, lo:hi], in_=zlast[:, lo:hi], func=ACT.Sigmoid)
-            cols = slice(3 * NCOL + lo, 3 * NCOL + hi)
-            nc.vector.tensor_tensor(out=hn_all[:, cols], in0=slast[:, lo:hi], in1=th[3][:, lo:hi], op=ALU.mult)
+        def last_sig(j):
+            sl = ep.tile([P, P], F32, name="sl", tag="sl", bufs=4)
+            nc.scalar.activation(out=sl[:], in_=state["zl%d" % j][:], func=ACT.Sigmoid)
+            state["sl%d" % j] = sl
+
+        def last_h(j):
+            cols = slice(3 * NCOL + j * P, 3 * NCOL + (j + 1) * P)
+            nc.vector.tensor_tensor(
+                out=hn_all[:, cols], in0=state["sl%d" % j][:], in1=th[3][:, j * P : (j + 1) * P], op=ALU.mult
+            )
             store(out_0[:, cols], hn_all[:, cols])
 
-        def last_z(r):
-            cols = slice((2 + r) * P, (3 + r) * P)
-            nc.vector.tensor_tensor(out=zlast[:, cols], in0=blk[r][:], in1=zlast[:, cols], op=ALU.add)
+        def loads_after(n):
+            ci, r = divmod(n, 8)
+            if ci < LAST and r % 4 == 3:
+                done = 2 * ci + r // 4
+            elif ci == LAST and r % 2 == 1:
+                done = 2 * LAST + r // 2
+            else:
+                return
+            if done + WBUFS < NLOADS:
+                load(done + WBUFS)
 
-        for k in range(NMAIN):
-            unit_t(k)
-            loads_after(k)
-            if k >= 1:
-                unit_q(k - 1)
-            if k == X_AT:
-                prepare_x()
-            if k == H_AT:
-                prepare_h()
-            if k == X_AT + 1:
-                quantise_act(0)
-            if k == H_AT + 1:
-                quantise_act(1)
-            if k == IG_AT:
+        NMAIN = 8 * LAST
+        xg = None
+        hgs = None
+        for n in range(NMAIN):
+            unit_t(n, "V" if n % 16 in V_COPIES else "S")
+            loads_after(n)
+            if n == 2:
+                xg = prepare_x()
+            if n == 4:
+                quantise(xg, act_codes[0][:], act_scales[0][:])
+            if n == 8:
+                hgs = prepare_h()
+            if n == 10:
+                for gp in range(2):
+                    cols = slice(gp * 256, (gp + 1) * 256)
+                    quantise(hgs[gp], act_codes[1][:, cols], act_scales[1][:, cols])
+            if n == 16:
                 prepare_ig()
-            for n in range(8):
-                if BIAS_AT[n] == k:
-                    spread_bias(n % 2, n // 2)
-            if k % 2 == 1 and k >= 3:
-                for m in (k - 3, k - 2):
-                    unit_mx(m)
-                    schedule_epilogue(k, m)
-            late(k)
+            if n in BIAS_AT:
+                spread_bias(BIAS_AT.index(n) % 2, BIAS_AT.index(n) // 2)
+            if n >= QLAG:
+                unit_q(n - QLAG)
+            m = n - MXLAG
+            if m >= 0 and m % 8 == 7:
+                chunk_mx(m // 8, (0, 1))
+            if m >= 4 and m % 8 == 3:
+                chunk_mx(m // 8 - 1, (2, 3))
+                schedule_epilogue(n, m // 8 - 1)
+            for fn in deferred.get(n, []):
+                fn()
 
-        unit_t(NMAIN, "SS")
+        def block_t(j):
+            for s in range(2):
+                unit_t(NMAIN + 2 * j + s, "SS"[s])
+                loads_after(NMAIN + 2 * j + s)
+
+        def late(n):
+            for fn in deferred.get(n, []):
+                fn()
+
+        block_t(0)
+        unit_q(NMAIN - 2)
         unit_q(NMAIN - 1)
         late(NMAIN)
-        unit_t(NMAIN + 1, "SS")
-        for m in range(NMAIN - END_BACK, NMAIN):
-            unit_mx(m)
-        unit_q(NMAIN)
-        unit_mx(NMAIN)
-        last_zpart()
-        unit_q(NMAIN + 1)
-        unit_mx(NMAIN + 1)
-        last_z(0)
         late(NMAIN + 1)
+        chunk_mx(LAST - 2, (2, 3))
+        schedule_epilogue(NMAIN + 1, LAST - 2)
+        block_t(1)
+        unit_q(NMAIN)
+        unit_q(NMAIN + 1)
         late(NMAIN + 2)
         late(NMAIN + 3)
-        last_out(0, 384)
-        last_z(1)
-        last_out(384, 512)
+        chunk_mx(LAST - 1)
+        block_t(2)
+        unit_q(NMAIN + 2)
+        unit_q(NMAIN + 3)
+        late(NMAIN + 4)
+        late(NMAIN + 5)
+        ep_z(3, 1)
+        keep_zpart()
+        block_t(3)
+        unit_q(NMAIN + 4)
+        unit_q(NMAIN + 5)
+        late(NMAIN + 6)
+        late(NMAIN + 7)
+        for j in range(3):
+            block_mx(j)
+        unit_q(NMAIN + 6)
+        unit_q(NMAIN + 7)
+        block_mx(3)
+        for j in range(3):
+            last_z(j)
+            last_sig(j)
+        for j in range(3):
+            last_h(j)
+        last_z(3)
+        last_sig(3)
+        last_h(3)

@@ -47,7 +47,7 @@ def tile_naivelstm_pb_kernel(
         cpool = ctx.enter_context(tc.tile_pool(name="cpool", bufs=3))
         ep = ctx.enter_context(tc.tile_pool(name="ep", bufs=2))
         accp = ctx.enter_context(tc.psum_pool(name="accp", bufs=1))
-        tp = ctx.enter_context(tc.psum_pool(name="tp", bufs=6))
+        tp = ctx.enter_context(tc.psum_pool(name="tp", bufs=3))
 
         w_views = [
             w.rearrange("(a q s r) k -> a s q (r k)", a=4, q=P, s=2, r=2)
@@ -113,18 +113,29 @@ def tile_naivelstm_pb_kernel(
         for n in range(5, WBUFS):
             load(n)
 
+        pair = {"tile": None, "used": 2}
+
+        def new_bank():
+            if pair["used"] == 2:
+                pair["tile"] = tp.tile([P, 2, NCOL], F32, name="xt", tag="xt")
+                pair["used"] = 0
+            bank = pair["tile"][:, pair["used"], :]
+            pair["used"] = pair["used"] + 1
+            return bank
+
         def transpose_bank(src32, cols):
-            bank = tp.tile([P, 2, 2, P], F32, name="xt", tag="xt")
+            bank = new_bank()
             for u in range(2):
                 for s in range(2):
                     col = cols[u][s]
-                    nc.tensor.transpose(bank[:, u, s, :], src32[:, col : col + P], ident32[:])
+                    at = (2 * u + s) * P
+                    nc.tensor.transpose(bank[:, at : at + P], src32[:, col : col + P], ident32[:])
             return bank
 
         def copy_bank(eng, bank):
             grouped = gpool.tile([P, K // 2], BF16, name="grouped", tag="grouped", align_bytes=64)
             dst = grouped[:].bitcast(F32).rearrange("p (n u) -> p n u", u=2)
-            src = bank[:].rearrange("p u s q -> p (s q) u")
+            src = bank.rearrange("p (u n) -> p n u", u=2)
             if eng == "S":
                 nc.scalar.copy(out=dst, in_=src)
             else:
@@ -159,24 +170,24 @@ def tile_naivelstm_pb_kernel(
         igT = const.tile([P, 4, 4, P], BF16, name="igT")
 
         def prepare_ig():
+            ibanks = tp.tile([P, 2, 2, 4, P], BF16, name="ibanks", tag="xt")
             for half in range(2):
-                ibank = tp.tile([P, 2, 4, P], BF16, name="ibank", tag="xt")
                 for a2 in range(2):
                     for j in range(4):
                         nc.tensor.transpose(
-                            ibank[:, a2, j, :],
+                            ibanks[:, half, a2, j, :],
                             ig_sb[:, 2 * half + a2, j * P : (j + 1) * P],
                             identb[:],
                         )
-                nc.scalar.copy(out=igT[:, 2 * half : 2 * half + 2, :, :], in_=ibank[:])
+                nc.scalar.copy(out=igT[:, 2 * half : 2 * half + 2, :, :], in_=ibanks[:, half, :, :, :])
 
         bias = const.tile([P, 2 * HID], F32, name="bias")
 
         def spread_bias(gate, a):
             cols = slice(gate * HID + a * NCOL, gate * HID + (a + 1) * NCOL)
-            bbank = tp.tile([P, NCOL], F32, name="bbank", tag="xt")
-            nc.tensor.matmul(out=bbank[:], lhsT=ones[:], rhs=brow[:, cols], start=True, stop=True)
-            nc.scalar.copy(out=bias[:, cols], in_=bbank[:])
+            bbank = new_bank()
+            nc.tensor.matmul(out=bbank, lhsT=ones[:], rhs=brow[:, cols], start=True, stop=True)
+            nc.scalar.copy(out=bias[:, cols], in_=bbank)
 
         cn_all = const.tile([P, HID], F32, name="cn_all")
         hn_all = const.tile([P, HID], F32, name="hn_all")
@@ -226,22 +237,22 @@ def tile_naivelstm_pb_kernel(
                 stop=stop,
             )
 
-        def chunk_mx(ci, passes=(0, 1, 2, 3)):
+        def chunk_mx(ci):
             wsel, a = CHUNKS[ci]
             gate, opnd = divmod(wsel, 2)
             alone = (wsel, a) == (2, 3)
-            if opnd == 0 and passes[0] == 0:
+            if opnd == 0:
                 acc[gate] = accp.tile([P, NCOL], F32, name="acc%d" % gate, tag="acc%d" % gate)
-            for g in passes:
+            for g in range(4):
                 mx(acc[gate][:], opnd, g, ci, g, slice(0, NCOL), opnd == 0 and g == 0, (opnd == 1 or alone) and g == 3)
 
         def block_mx(j):
             if j < 2:
-                blk[j] = accp.tile([P, P], F32, name="acc%d" % j, tag="acc%d" % j)
+                blk[j] = accp.tile([P, P], F32, name="acc%d" % j, tag="acc%d" % j)[:]
             else:
-                blk[j] = tp.tile([P, P], F32, name="blk", tag="xt")
+                blk[j] = new_bank()[:, 0:P]
             for g in range(4):
-                mx(blk[j][:], 1, g, LAST, j, slice(g * P, (g + 1) * P), g == 0, g == 3)
+                mx(blk[j], 1, g, LAST, j, slice(g * P, (g + 1) * P), g == 0, g == 3)
 
         def natural(ap):
             return ap.rearrange("p (q j) -> p q j", j=4)
@@ -304,7 +315,7 @@ def tile_naivelstm_pb_kernel(
         def last_z(j):
             zl = ep.tile([P, P], F32, name="zl", tag="zl", bufs=4)
             nc.vector.tensor_tensor(
-                out=zl[:], in0=blk[j][:], in1=state["zpart"][:, j * P : (j + 1) * P], op=ALU.add
+                out=zl[:], in0=blk[j], in1=state["zpart"][:, j * P : (j + 1) * P], op=ALU.add
             )
             state["zl%d" % j] = zl
 
@@ -355,10 +366,8 @@ def tile_naivelstm_pb_kernel(
                 unit_q(n - QLAG)
             m = n - MXLAG
             if m >= 0 and m % 8 == 7:
-                chunk_mx(m // 8, (0, 1))
-            if m >= 4 and m % 8 == 3:
-                chunk_mx(m // 8 - 1, (2, 3))
-                schedule_epilogue(n, m // 8 - 1)
+                chunk_mx(m // 8)
+                schedule_epilogue(n, m // 8)
             for fn in deferred.get(n, []):
                 fn()
 
@@ -376,8 +385,6 @@ def tile_naivelstm_pb_kernel(
         unit_q(NMAIN - 1)
         late(NMAIN)
         late(NMAIN + 1)
-        chunk_mx(LAST - 2, (2, 3))
-        schedule_epilogue(NMAIN + 1, LAST - 2)
         block_t(1)
         unit_q(NMAIN)
         unit_q(NMAIN + 1)
@@ -394,8 +401,6 @@ def tile_naivelstm_pb_kernel(
         block_t(3)
         unit_q(NMAIN + 4)
         unit_q(NMAIN + 5)
-        late(NMAIN + 6)
-        late(NMAIN + 7)
         for j in range(3):
             block_mx(j)
         unit_q(NMAIN + 6)

@@ -21,7 +21,12 @@ QLAG = 2
 MXLAG = 6
 V_COPIES = (3, 8, 13)
 EARLY_STORES = 0
-BIAS_AT = (9, 10, 11, 12, 13, 14, 15, 17)
+BIAS_AT = (7, 7, 7, 7, 7, 7, 7, 7)
+SMALL_LOADS = (("x", 2), ("h", 4), ("ig", 13), ("c", 14))
+X_AT = 6
+H_AT = 15
+IG_AT = 57
+C_AT = 62
 
 FLOPS = 2 * 4 * 2048 * 2048 * 128
 
@@ -47,7 +52,7 @@ def tile_naivelstm_pb_kernel(
         cpool = ctx.enter_context(tc.tile_pool(name="cpool", bufs=3))
         ep = ctx.enter_context(tc.tile_pool(name="ep", bufs=2))
         accp = ctx.enter_context(tc.psum_pool(name="accp", bufs=1))
-        tp = ctx.enter_context(tc.psum_pool(name="tp", bufs=3))
+        tp = ctx.enter_context(tc.psum_pool(name="tp", bufs=6))
 
         w_views = [
             w.rearrange("(a q s r) k -> a s q (r k)", a=4, q=P, s=2, r=2)
@@ -56,21 +61,56 @@ def tile_naivelstm_pb_kernel(
 
         ident32 = const.tile([P, P], F32, name="ident32")
         identb = const.tile([P, P], BF16, name="identb")
-        ones = const.tile([P, P], BF16, name="ones")
-        brow = const.tile([P, 2 * HID], BF16, name="brow")
-        nc.vector.memset(brow[:].bitcast(I32), 0)
-        make_identity(nc, ident32[:])
+        brows = const.tile([P, NCOL], BF16, name="brows")
+        nc.vector.memset(brows[:].bitcast(I32), 0)
+        for first_row, b in ((0, b_if), (1, b_hf), (2, b_io), (3, b_ho)):
+            nc.scalar.dma_start(
+                out=brows[first_row : 16 : 4, :], in_=b.rearrange("(a n) o -> a (n o)", a=4)
+            )
         make_identity(nc, identb[:])
-        nc.gpsimd.memset(ones[:], 1.0)
+        make_identity(nc, ident32[:])
+        pairsel = const.tile([P, 8], BF16, name="pairsel")
+        nc.vector.tensor_tensor(out=pairsel[:], in0=identb[:, 0:16:2], in1=identb[:, 1:16:2], op=ALU.add)
         warm = const.tile([P, 2], F32, name="warm")
         nc.vector.memset(warm[:], 0.0)
         nc.scalar.activation(out=warm[:, 1:2], in_=warm[:, 0:1], func=ACT.Sigmoid)
 
         NLOADS = 2 * LAST + 4
         wt = {}
+        first = {}
         stores = {"open": False, "early": EARLY_STORES, "pending": []}
 
+        h_sb = const.tile([P, K], BF16, name="h_sb")
+        xraw = const.tile([P, 8, 2, P], BF16, name="xraw")
+        ig_sb = const.tile([P, 4, 4 * P], BF16, name="ig_sb")
+        c_sb = const.tile([P, HID], BF16, name="c_sb")
+
+        def small_load(what):
+            if what == "x":
+                nc.sync.dma_start(out=xraw[:], in_=x.rearrange("(s p e) b -> p s e b", s=8, p=P, e=2))
+            elif what == "h":
+                nc.sync.dma_start(out=h_sb[:], in_=h)
+            elif what == "ig":
+                nc.sync.dma_start(out=ig_sb[:], in_=ig.rearrange("(a q j) b -> q a (j b)", a=4, q=P, j=4))
+            else:
+                nc.sync.dma_start(out=c_sb[:], in_=c)
+
         def load(n):
+            for what, before in SMALL_LOADS:
+                if before == n:
+                    small_load(what)
+            if n == 0:
+                wsel, a = CHUNKS[0]
+                for g in range(2):
+                    t = const.tile([P, 2, K // 2], BF16, name="first%d" % g)
+                    nc.sync.dma_start(
+                        out=t[:],
+                        in_=(w_if, w_hf, w_io, w_ho)[wsel].rearrange("(a q s r) k -> a s q r k", a=4, q=P, s=2, r=2)[
+                            a, 0, :, :, g * (K // 2) : (g + 1) * (K // 2)
+                        ],
+                    )
+                    first[g] = t
+                return
             if n < 2 * LAST:
                 t = wpool.tile([P, 2 * K], BF16, name="wt", tag="wt")
                 wsel, a = CHUNKS[n // 2]
@@ -92,50 +132,21 @@ def tile_naivelstm_pb_kernel(
             else:
                 stores["pending"].append((dst, src))
 
-        h_sb = const.tile([P, K], BF16, name="h_sb")
-        xraw = const.tile([P, 8, 2, P], BF16, name="xraw")
-        ig_sb = const.tile([P, 4, 4 * P], BF16, name="ig_sb")
-        c_sb = const.tile([P, HID], BF16, name="c_sb")
-        for row, gate, b in ((0, 0, b_if), (1, 0, b_hf), (0, 1, b_io), (1, 1, b_ho)):
-            nc.scalar.dma_start(
-                out=brow[row : row + 1, gate * HID : (gate + 1) * HID],
-                in_=b.rearrange("n o -> o n"),
-            )
-        load(0)
-        nc.sync.dma_start(out=xraw[:], in_=x.rearrange("(s p e) b -> p s e b", s=8, p=P, e=2))
-        load(1)
-        nc.sync.dma_start(out=h_sb[:], in_=h)
-        load(2)
-        load(3)
-        nc.sync.dma_start(out=ig_sb[:], in_=ig.rearrange("(a q j) b -> q a (j b)", a=4, q=P, j=4))
-        load(4)
-        nc.sync.dma_start(out=c_sb[:], in_=c)
-        for n in range(5, WBUFS):
+        for n in range(WBUFS + 1):
             load(n)
 
-        pair = {"tile": None, "used": 2}
-
-        def new_bank():
-            if pair["used"] == 2:
-                pair["tile"] = tp.tile([P, 2, NCOL], F32, name="xt", tag="xt")
-                pair["used"] = 0
-            bank = pair["tile"][:, pair["used"], :]
-            pair["used"] = pair["used"] + 1
-            return bank
-
         def transpose_bank(src32, cols):
-            bank = new_bank()
+            bank = tp.tile([P, 2, 2, P], F32, name="xt", tag="xt")
             for u in range(2):
                 for s in range(2):
                     col = cols[u][s]
-                    at = (2 * u + s) * P
-                    nc.tensor.transpose(bank[:, at : at + P], src32[:, col : col + P], ident32[:])
+                    nc.tensor.transpose(bank[:, u, s, :], src32[:, col : col + P], ident32[:])
             return bank
 
         def copy_bank(eng, bank):
             grouped = gpool.tile([P, K // 2], BF16, name="grouped", tag="grouped", align_bytes=64)
             dst = grouped[:].bitcast(F32).rearrange("p (n u) -> p n u", u=2)
-            src = bank.rearrange("p (u n) -> p n u", u=2)
+            src = bank[:].rearrange("p u s q -> p (s q) u")
             if eng == "S":
                 nc.scalar.copy(out=dst, in_=src)
             else:
@@ -170,24 +181,30 @@ def tile_naivelstm_pb_kernel(
         igT = const.tile([P, 4, 4, P], BF16, name="igT")
 
         def prepare_ig():
-            ibanks = tp.tile([P, 2, 2, 4, P], BF16, name="ibanks", tag="xt")
             for half in range(2):
+                ibank = tp.tile([P, 2, 4, P], BF16, name="ibank", tag="xt")
                 for a2 in range(2):
                     for j in range(4):
                         nc.tensor.transpose(
-                            ibanks[:, half, a2, j, :],
+                            ibank[:, a2, j, :],
                             ig_sb[:, 2 * half + a2, j * P : (j + 1) * P],
                             identb[:],
                         )
-                nc.scalar.copy(out=igT[:, 2 * half : 2 * half + 2, :, :], in_=ibanks[:, half, :, :, :])
+                nc.scalar.copy(out=igT[:, 2 * half : 2 * half + 2, :, :], in_=ibank[:])
 
         bias = const.tile([P, 2 * HID], F32, name="bias")
 
         def spread_bias(gate, a):
             cols = slice(gate * HID + a * NCOL, gate * HID + (a + 1) * NCOL)
-            bbank = new_bank()
-            nc.tensor.matmul(out=bbank, lhsT=ones[:], rhs=brow[:, cols], start=True, stop=True)
-            nc.scalar.copy(out=bias[:, cols], in_=bbank)
+            bbank = tp.tile([P, NCOL], F32, name="bbank", tag="xt")
+            i = 2 * a + gate
+            nc.tensor.matmul(
+                out=bbank[:], lhsT=pairsel[:, i : i + 1].to_broadcast([P, P]), rhs=brows[:], start=True, stop=True
+            )
+            if gate == 0:
+                nc.scalar.copy(out=bias[:, cols], in_=bbank[:])
+            else:
+                nc.vector.tensor_copy(out=bias[:, cols], in_=bbank[:])
 
         cn_all = const.tile([P, HID], F32, name="cn_all")
         hn_all = const.tile([P, HID], F32, name="hn_all")
@@ -205,12 +222,15 @@ def tile_naivelstm_pb_kernel(
 
         def unit_t(n, eng):
             ci, r = divmod(n, 8)
-            first, second = divmod(r, 4) if ci < LAST else divmod(r, 2)
-            if ci < LAST:
-                w32 = wt[2 * ci + first][:].bitcast(F32)
+            half, second = divmod(r, 4) if ci < LAST else divmod(r, 2)
+            if n < 4:
+                w32 = first[n // 2][:].rearrange("p r k -> p (r k)").bitcast(F32)
+                cols = [[s * 512 + (2 * (n % 2) + u) * P for s in range(2)] for u in range(2)]
+            elif ci < LAST:
+                w32 = wt[2 * ci + half][:].bitcast(F32)
                 cols = [[s * 1024 + (2 * second + u) * P for s in range(2)] for u in range(2)]
             else:
-                w32 = wt[2 * LAST + first][:].bitcast(F32)
+                w32 = wt[2 * LAST + half][:].bitcast(F32)
                 cols = row_block_cols(second)
             grouped[n] = copy_bank(eng, transpose_bank(w32, cols))
 
@@ -248,11 +268,11 @@ def tile_naivelstm_pb_kernel(
 
         def block_mx(j):
             if j < 2:
-                blk[j] = accp.tile([P, P], F32, name="acc%d" % j, tag="acc%d" % j)[:]
+                blk[j] = accp.tile([P, P], F32, name="acc%d" % j, tag="acc%d" % j)
             else:
-                blk[j] = new_bank()[:, 0:P]
+                blk[j] = tp.tile([P, P], F32, name="blk", tag="xt")
             for g in range(4):
-                mx(blk[j], 1, g, LAST, j, slice(g * P, (g + 1) * P), g == 0, g == 3)
+                mx(blk[j][:], 1, g, LAST, j, slice(g * P, (g + 1) * P), g == 0, g == 3)
 
         def natural(ap):
             return ap.rearrange("p (q j) -> p q j", j=4)
@@ -267,15 +287,15 @@ def tile_naivelstm_pb_kernel(
             )
             state["z"] = z
 
-        def ep_sig():
-            s = ep.tile([P, NCOL], F32, name="sg", tag="sg")
+        def ep_sig(a, gate):
+            s = ep.tile([P, NCOL], F32, name="sg", tag="sg", bufs=4)
             nc.scalar.activation(out=s[:], in_=state["z"][:], func=ACT.Sigmoid)
-            state["s"] = s
+            state[(gate, a)] = s
 
         def ep_cnext(a):
             cols = slice(a * NCOL, (a + 1) * NCOL)
             t = ep.tile([P, NCOL], F32, name="fc", tag="fc")
-            nc.vector.tensor_tensor(out=t[:], in0=state["s"][:], in1=c_sb[:, cols], op=ALU.mult)
+            nc.vector.tensor_tensor(out=t[:], in0=state[(0, a)][:], in1=c_sb[:, cols], op=ALU.mult)
             nc.vector.tensor_tensor(
                 out=natural(cn_all[:, cols]),
                 in0=natural(t[:]),
@@ -291,7 +311,7 @@ def tile_naivelstm_pb_kernel(
 
         def ep_hnext(a):
             cols = slice(a * NCOL, (a + 1) * NCOL)
-            nc.vector.tensor_tensor(out=hn_all[:, cols], in0=state["s"][:], in1=th[a][:], op=ALU.mult)
+            nc.vector.tensor_tensor(out=hn_all[:, cols], in0=state[(1, a)][:], in1=th[a][:], op=ALU.mult)
             store(out_0[:, cols], hn_all[:, cols])
 
         def keep_zpart():
@@ -301,13 +321,13 @@ def tile_naivelstm_pb_kernel(
             wsel, a = CHUNKS[ci]
             if wsel == 1:
                 defer(slot + 1, lambda: ep_z(a, 0))
-                defer(slot + 3, ep_sig)
-                defer(slot + 5, lambda: ep_cnext(a))
-                defer(slot + 7, lambda: ep_tanh(a))
+                defer(slot + 3, lambda: ep_sig(a, 0))
+                defer(max(slot + 5, C_AT), lambda: ep_cnext(a))
+                defer(max(slot + 7, C_AT + 2), lambda: ep_tanh(a))
             if wsel == 3:
                 defer(slot + 1, lambda: ep_z(a, 1))
-                defer(slot + 3, ep_sig)
-                defer(slot + 5, lambda: ep_hnext(a))
+                defer(slot + 3, lambda: ep_sig(a, 1))
+                defer(max(slot + 5, C_AT + 4), lambda: ep_hnext(a))
             if (wsel, a) == (2, 3):
                 defer(slot + 1, lambda: ep_z(a, 1))
                 defer(slot + 1, keep_zpart)
@@ -315,7 +335,7 @@ def tile_naivelstm_pb_kernel(
         def last_z(j):
             zl = ep.tile([P, P], F32, name="zl", tag="zl", bufs=4)
             nc.vector.tensor_tensor(
-                out=zl[:], in0=blk[j], in1=state["zpart"][:, j * P : (j + 1) * P], op=ALU.add
+                out=zl[:], in0=blk[j][:], in1=state["zpart"][:, j * P : (j + 1) * P], op=ALU.add
             )
             state["zl%d" % j] = zl
 
@@ -339,7 +359,7 @@ def tile_naivelstm_pb_kernel(
                 done = 2 * LAST + r // 2
             else:
                 return
-            if done + WBUFS < NLOADS:
+            if done >= 1 and done + WBUFS < NLOADS:
                 load(done + WBUFS)
 
         NMAIN = 8 * LAST
@@ -348,20 +368,21 @@ def tile_naivelstm_pb_kernel(
         for n in range(NMAIN):
             unit_t(n, "V" if n % 16 in V_COPIES else "S")
             loads_after(n)
-            if n == 2:
+            if n == X_AT:
                 xg = prepare_x()
-            if n == 4:
+            if n == X_AT + 2:
                 quantise(xg, act_codes[0][:], act_scales[0][:])
-            if n == 8:
+            if n == H_AT:
                 hgs = prepare_h()
-            if n == 10:
+            if n == H_AT + 2:
                 for gp in range(2):
                     cols = slice(gp * 256, (gp + 1) * 256)
                     quantise(hgs[gp], act_codes[1][:, cols], act_scales[1][:, cols])
-            if n == 16:
+            if n == IG_AT:
                 prepare_ig()
-            if n in BIAS_AT:
-                spread_bias(BIAS_AT.index(n) % 2, BIAS_AT.index(n) // 2)
+            for i in range(8):
+                if BIAS_AT[i] == n:
+                    spread_bias(i % 2, i // 2)
             if n >= QLAG:
                 unit_q(n - QLAG)
             m = n - MXLAG
@@ -409,8 +430,9 @@ def tile_naivelstm_pb_kernel(
         for j in range(3):
             last_z(j)
             last_sig(j)
-        for j in range(3):
-            last_h(j)
+        last_h(0)
+        last_h(1)
         last_z(3)
         last_sig(3)
+        last_h(2)
         last_h(3)

@@ -16,17 +16,15 @@ P = 128
 K = 2048
 HID = 2048
 NCOL = 512
-WBUFS = 10
-QLAG = 2
-MXLAG = 6
-V_COPIES = (3, 8, 13)
-EARLY_STORES = 0
-BIAS_AT = (7, 7, 7, 7, 7, 7, 7, 7)
-SMALL_LOADS = (("x", 2), ("h", 4), ("ig", 13), ("c", 14))
-X_AT = 6
-H_AT = 15
-IG_AT = 57
-C_AT = 62
+WBUFS = 6
+V_BANKS = (1, 5)
+V_BANKS_EARLY = (1, 5)
+EARLY_UNITS = 6
+SPLIT_CHUNKS = ()
+BIAS_AT = (2, 2, 3, 3, 4, 4, 5, 5)
+X_AT = 1
+H_AT = 2
+IG_AT = 4
 
 FLOPS = 2 * 4 * 2048 * 2048 * 128
 
@@ -36,8 +34,8 @@ CHUNKS = (
     (0, 2), (1, 2), (0, 3), (1, 3),
     (2, 2), (3, 2), (2, 3), (3, 3),
 )
-NCH = len(CHUNKS)
-LAST = NCH - 1
+ACC_BANK = {(0, 0): 0, (1, 0): 1, (0, 1): 0, (1, 1): 1, (0, 2): 0, (0, 3): 1, (1, 2): 0, (1, 3): 1}
+LAST = len(CHUNKS) - 1
 
 
 def tile_naivelstm_pb_kernel(
@@ -48,16 +46,13 @@ def tile_naivelstm_pb_kernel(
         ctx.enter_context(tc.manual_schedule())
         const = ctx.enter_context(tc.tile_pool(name="const", bufs=1))
         wpool = ctx.enter_context(tc.tile_pool(name="wpool", bufs=WBUFS))
-        gpool = ctx.enter_context(tc.tile_pool(name="gpool", bufs=8))
-        cpool = ctx.enter_context(tc.tile_pool(name="cpool", bufs=3))
+        gpool = ctx.enter_context(tc.tile_pool(name="gpool", bufs=3))
+        cpool = ctx.enter_context(tc.tile_pool(name="cpool", bufs=6))
         ep = ctx.enter_context(tc.tile_pool(name="ep", bufs=2))
         accp = ctx.enter_context(tc.psum_pool(name="accp", bufs=1))
         tp = ctx.enter_context(tc.psum_pool(name="tp", bufs=6))
 
-        w_views = [
-            w.rearrange("(a q s r) k -> a s q (r k)", a=4, q=P, s=2, r=2)
-            for w in (w_if, w_hf, w_io, w_ho)
-        ]
+        weights = (w_if, w_hf, w_io, w_ho)
 
         ident32 = const.tile([P, P], F32, name="ident32")
         identb = const.tile([P, P], BF16, name="identb")
@@ -75,65 +70,85 @@ def tile_naivelstm_pb_kernel(
         nc.vector.memset(warm[:], 0.0)
         nc.scalar.activation(out=warm[:, 1:2], in_=warm[:, 0:1], func=ACT.Sigmoid)
 
-        NLOADS = 2 * LAST + 4
-        wt = {}
-        first = {}
-        stores = {"open": False, "early": EARLY_STORES, "pending": []}
-
-        h_sb = const.tile([P, K], BF16, name="h_sb")
-        xraw = const.tile([P, 8, 2, P], BF16, name="xraw")
-        ig_sb = const.tile([P, 4, 4 * P], BF16, name="ig_sb")
-        c_sb = const.tile([P, HID], BF16, name="c_sb")
-
-        def small_load(what):
-            if what == "x":
-                nc.sync.dma_start(out=xraw[:], in_=x.rearrange("(s p e) b -> p s e b", s=8, p=P, e=2))
-            elif what == "h":
-                nc.sync.dma_start(out=h_sb[:], in_=h)
-            elif what == "ig":
-                nc.sync.dma_start(out=ig_sb[:], in_=ig.rearrange("(a q j) b -> q a (j b)", a=4, q=P, j=4))
+        loads = []
+        units = []
+        for ci in range(LAST):
+            if ci in SPLIT_CHUNKS:
+                for gp in range(2):
+                    units.append((len(loads), "half", ci, gp))
+                    loads.append(("half", ci, gp))
             else:
-                nc.sync.dma_start(out=c_sb[:], in_=c)
+                for gp in range(2):
+                    units.append((len(loads), "whole", ci, gp))
+                loads.append(("whole", ci, 0))
+        NMAIN = len(units)
+        for j in range(4):
+            units.append((len(loads), "block", LAST, j))
+            loads.append(("block", LAST, j))
+        last_unit_of_load = {}
+        for k in range(len(units)):
+            last_unit_of_load[units[k][0]] = k
+
+        wt = {}
+        stores = {"open": False, "pending": []}
 
         def load(n):
-            for what, before in SMALL_LOADS:
-                if before == n:
-                    small_load(what)
-            if n == 0:
-                wsel, a = CHUNKS[0]
-                for g in range(2):
-                    t = const.tile([P, 2, K // 2], BF16, name="first%d" % g)
-                    nc.sync.dma_start(
-                        out=t[:],
-                        in_=(w_if, w_hf, w_io, w_ho)[wsel].rearrange("(a q s r) k -> a s q r k", a=4, q=P, s=2, r=2)[
-                            a, 0, :, :, g * (K // 2) : (g + 1) * (K // 2)
-                        ],
-                    )
-                    first[g] = t
-                return
-            if n < 2 * LAST:
-                t = wpool.tile([P, 2 * K], BF16, name="wt", tag="wt")
-                wsel, a = CHUNKS[n // 2]
-                nc.sync.dma_start(out=t[:], in_=w_views[wsel][a, n % 2, :, :])
+            kind, ci, part = loads[n]
+            wsel, a = CHUNKS[ci]
+            w = weights[wsel]
+            if kind == "whole":
+                t = wpool.tile([P, 4 * K], BF16, name="wt", tag="wt")
+                nc.sync.dma_start(
+                    out=t[:], in_=w.rearrange("(a q j) k -> a q (j k)", a=4, q=P, j=4)[a, :, :]
+                )
+            elif kind == "half":
+                t = wpool.tile([P, 4, K // 2], BF16, name="wt", tag="wt")
+                nc.sync.dma_start(
+                    out=t[:],
+                    in_=w.rearrange("(a q j) k -> a q j k", a=4, q=P, j=4)[
+                        a, :, :, part * (K // 2) : (part + 1) * (K // 2)
+                    ],
+                )
             else:
-                j = n - 2 * LAST
                 t = wpool.tile([P, K], BF16, name="wt", tag="wt")
-                nc.sync.dma_start(out=t[:], in_=w_ho[3 * NCOL + j * P : 3 * NCOL + (j + 1) * P, :])
+                nc.sync.dma_start(out=t[:], in_=w[a * NCOL + part * P : a * NCOL + (part + 1) * P, :])
             wt[n] = t
-            if n == NLOADS - 1:
+            if n == len(loads) - 1:
                 stores["open"] = True
                 for dst, src in stores["pending"]:
                     nc.sync.dma_start(out=dst, in_=src)
 
         def store(dst, src):
-            if stores["open"] or stores["early"] > 0:
-                stores["early"] = stores["early"] - 1
+            if stores["open"]:
                 nc.sync.dma_start(out=dst, in_=src)
             else:
                 stores["pending"].append((dst, src))
 
-        for n in range(WBUFS + 1):
-            load(n)
+        h_sb = const.tile([P, K], BF16, name="h_sb")
+        xraw = const.tile([P, 8, 2, P], BF16, name="xraw")
+        ig_sb = const.tile([P, 4, 4 * P], BF16, name="ig_sb")
+        c_sb = const.tile([P, HID], BF16, name="c_sb")
+        load(0)
+        nc.sync.dma_start(out=xraw[:], in_=x.rearrange("(s p e) b -> p s e b", s=8, p=P, e=2))
+        load(1)
+        nc.sync.dma_start(out=h_sb[:], in_=h)
+        load(2)
+        nc.sync.dma_start(out=ig_sb[:], in_=ig.rearrange("(a q j) b -> q a (j b)", a=4, q=P, j=4))
+        nc.sync.dma_start(out=c_sb[:], in_=c)
+        load(3)
+        load(4)
+        progress = {"loaded": 5, "freed": 0}
+
+        def loads_after(k):
+            if last_unit_of_load[units[k][0]] == k:
+                progress["freed"] = progress["freed"] + 1
+            while progress["loaded"] < len(loads) and progress["loaded"] - progress["freed"] < WBUFS:
+                load(progress["loaded"])
+                progress["loaded"] = progress["loaded"] + 1
+
+        while progress["loaded"] < WBUFS:
+            load(progress["loaded"])
+            progress["loaded"] = progress["loaded"] + 1
 
         def transpose_bank(src32, cols):
             bank = tp.tile([P, 2, 2, P], F32, name="xt", tag="xt")
@@ -143,18 +158,14 @@ def tile_naivelstm_pb_kernel(
                     nc.tensor.transpose(bank[:, u, s, :], src32[:, col : col + P], ident32[:])
             return bank
 
-        def copy_bank(eng, bank):
-            grouped = gpool.tile([P, K // 2], BF16, name="grouped", tag="grouped", align_bytes=64)
+        def copy_bank(eng, grouped, slot, bank):
             dst = grouped[:].bitcast(F32).rearrange("p (n u) -> p n u", u=2)
+            dst = dst[:, slot * 256 : (slot + 1) * 256, :]
             src = bank[:].rearrange("p u s q -> p (s q) u")
             if eng == "S":
                 nc.scalar.copy(out=dst, in_=src)
             else:
                 nc.vector.tensor_copy(out=dst, in_=src)
-            return grouped
-
-        def quantise(grouped, codes, scales):
-            nc.vector.quantize_mx(out=codes.bitcast(FP8X4), scales=scales, in_=grouped[:])
 
         def row_block_cols(gp):
             return [[(2 * (2 * gp + s) + u) * P for s in range(2)] for u in range(2)]
@@ -164,19 +175,28 @@ def tile_naivelstm_pb_kernel(
         for nm in ("x", "h"):
             act_codes.append(const.tile([P, 512], U32, name="codes_" + nm, align_bytes=64))
             act_scales.append(const.tile([P, 512], U8, name="scales_" + nm, align_bytes=64))
+        act_grouped = {}
 
         def prepare_x():
-            xg = const.tile([P, K], BF16, name="xg", align_bytes=64)
+            xg = gpool.tile([P, K], BF16, name="grouped", tag="grouped", align_bytes=64)
             nc.vector.tensor_copy(
                 out=xg[:].rearrange("p (g b t) -> p g b t", g=4, b=P, t=4),
                 in_=xraw[:].rearrange("p (g u) e b -> p g b (u e)", g=4, u=2),
             )
-            return xg
+            act_grouped[0] = xg
 
         def prepare_h():
             h32 = h_sb[:].bitcast(F32)
+            hg = gpool.tile([P, K], BF16, name="grouped", tag="grouped", align_bytes=64)
             hbanks = [transpose_bank(h32, row_block_cols(gp)) for gp in range(2)]
-            return [copy_bank("SV"[gp], hbanks[gp]) for gp in range(2)]
+            for gp in range(2):
+                copy_bank("SV"[gp], hg, gp, hbanks[gp])
+            act_grouped[1] = hg
+
+        def quantise_act(opnd):
+            nc.vector.quantize_mx(
+                out=act_codes[opnd][:].bitcast(FP8X4), scales=act_scales[opnd][:], in_=act_grouped[opnd][:]
+            )
 
         igT = const.tile([P, 4, 4, P], BF16, name="igT")
 
@@ -201,10 +221,7 @@ def tile_naivelstm_pb_kernel(
             nc.tensor.matmul(
                 out=bbank[:], lhsT=pairsel[:, i : i + 1].to_broadcast([P, P]), rhs=brows[:], start=True, stop=True
             )
-            if gate == 0:
-                nc.scalar.copy(out=bias[:, cols], in_=bbank[:])
-            else:
-                nc.vector.tensor_copy(out=bias[:, cols], in_=bbank[:])
+            nc.scalar.copy(out=bias[:, cols], in_=bbank[:])
 
         cn_all = const.tile([P, HID], F32, name="cn_all")
         hn_all = const.tile([P, HID], F32, name="hn_all")
@@ -216,43 +233,59 @@ def tile_naivelstm_pb_kernel(
         th = {}
         blk = {}
         deferred = {}
+        banks_done = {"n": 0}
 
         def defer(slot, fn):
             deferred[slot] = deferred.get(slot, []) + [fn]
 
-        def unit_t(n, eng):
-            ci, r = divmod(n, 8)
-            half, second = divmod(r, 4) if ci < LAST else divmod(r, 2)
-            if n < 4:
-                w32 = first[n // 2][:].rearrange("p r k -> p (r k)").bitcast(F32)
-                cols = [[s * 512 + (2 * (n % 2) + u) * P for s in range(2)] for u in range(2)]
-            elif ci < LAST:
-                w32 = wt[2 * ci + half][:].bitcast(F32)
-                cols = [[s * 1024 + (2 * second + u) * P for s in range(2)] for u in range(2)]
-            else:
-                w32 = wt[2 * LAST + half][:].bitcast(F32)
-                cols = row_block_cols(second)
-            grouped[n] = copy_bank(eng, transpose_bank(w32, cols))
+        def late(slot):
+            for fn in deferred.get(slot, []):
+                fn()
 
-        def unit_q(n):
-            ci, r = divmod(n, 8)
-            if r == 0:
-                codes[ci] = cpool.tile([P, 4, NCOL], U32, name="codes", tag="codes", align_bytes=64)
-                scales[ci] = cpool.tile([P, 4, NCOL], U8, name="scales", tag="scales", align_bytes=64)
-            if ci < LAST:
-                half, row = divmod(r, 4)
+        def unit_t(k, engines=None):
+            n, kind, ci, part = units[k]
+            w32 = wt[n][:]
+            if kind == "half":
+                w32 = w32.rearrange("p j k -> p (j k)")
+            w32 = w32.bitcast(F32)
+            if kind == "block":
+                grouped[k] = gpool.tile([P, K], BF16, name="grouped", tag="grouped", align_bytes=64)
+                colmaps = [row_block_cols(gp) for gp in range(2)]
             else:
-                row, half = divmod(r, 2)
-            cols = slice(half * 256, (half + 1) * 256)
-            quantise(grouped[n], codes[ci][:, row, cols], scales[ci][:, row, cols])
+                grouped[k] = gpool.tile([P, 2 * K], BF16, name="grouped", tag="grouped", align_bytes=64)
+                rowlen = 1024 if kind == "whole" else 512
+                first = 2 * part if kind == "whole" else 0
+                colmaps = [
+                    [[(2 * jp + s) * rowlen + (2 * (first + gg) + u) * P for s in range(2)] for u in range(2)]
+                    for gg in range(2)
+                    for jp in range(2)
+                ]
+            for slot in range(len(colmaps)):
+                bank = transpose_bank(w32, colmaps[slot])
+                if engines is None and k >= NMAIN - 1:
+                    eng = "S"
+                elif engines is None:
+                    eng = "V" if banks_done["n"] % 8 in (V_BANKS_EARLY if k < EARLY_UNITS else V_BANKS) else "S"
+                else:
+                    eng = engines[slot]
+                banks_done["n"] = banks_done["n"] + 1
+                copy_bank(eng, grouped[k], slot, bank)
 
-        def mx(out, opnd, g, ci, row, cols, start, stop):
+        def unit_q(k):
+            width = NCOL if units[k][1] == "block" else 2 * NCOL
+            codes[k] = cpool.tile([P, width], U32, name="codes", tag="codes", align_bytes=64)
+            scales[k] = cpool.tile([P, width], U8, name="scales", tag="scales", align_bytes=64)
+            nc.vector.quantize_mx(
+                out=codes[k][:].bitcast(FP8X4), scales=scales[k][:], in_=grouped[k][:]
+            )
+
+        def mx(out, opnd, g, k, cols, start, stop):
             nc.tensor.matmul_mx(
                 out=out,
                 lhsT=act_codes[opnd][:, g * P : (g + 1) * P].bitcast(FP8X4),
                 lhsT_scale=act_scales[opnd][:, g * P : (g + 1) * P],
-                rhs=codes[ci][:, row, cols].bitcast(FP8X4),
-                rhs_scale=scales[ci][:, row, cols],
+                rhs=codes[k][:, cols].bitcast(FP8X4),
+                rhs_scale=scales[k][:, cols],
                 start=start,
                 stop=stop,
             )
@@ -262,17 +295,21 @@ def tile_naivelstm_pb_kernel(
             gate, opnd = divmod(wsel, 2)
             alone = (wsel, a) == (2, 3)
             if opnd == 0:
-                acc[gate] = accp.tile([P, NCOL], F32, name="acc%d" % gate, tag="acc%d" % gate)
+                bank = ACC_BANK[(gate, a)]
+                acc[gate] = accp.tile([P, NCOL], F32, name="acc%d" % bank, tag="acc%d" % bank)
             for g in range(4):
-                mx(acc[gate][:], opnd, g, ci, g, slice(0, NCOL), opnd == 0 and g == 0, (opnd == 1 or alone) and g == 3)
+                mx(
+                    acc[gate][:], opnd, g, 2 * ci + g // 2, slice((g % 2) * NCOL, (g % 2 + 1) * NCOL),
+                    opnd == 0 and g == 0, (opnd == 1 or alone) and g == 3,
+                )
 
         def block_mx(j):
-            if j < 2:
-                blk[j] = accp.tile([P, P], F32, name="acc%d" % j, tag="acc%d" % j)
+            if j == 0:
+                blk[j] = accp.tile([P, P], F32, name="acc0", tag="acc0")
             else:
                 blk[j] = tp.tile([P, P], F32, name="blk", tag="xt")
             for g in range(4):
-                mx(blk[j][:], 1, g, LAST, j, slice(g * P, (g + 1) * P), g == 0, g == 3)
+                mx(blk[j][:], 1, g, NMAIN + j, slice(g * P, (g + 1) * P), g == 0, g == 3)
 
         def natural(ap):
             return ap.rearrange("p (q j) -> p q j", j=4)
@@ -287,15 +324,15 @@ def tile_naivelstm_pb_kernel(
             )
             state["z"] = z
 
-        def ep_sig(a, gate):
-            s = ep.tile([P, NCOL], F32, name="sg", tag="sg", bufs=4)
+        def ep_sig():
+            s = ep.tile([P, NCOL], F32, name="sg", tag="sg")
             nc.scalar.activation(out=s[:], in_=state["z"][:], func=ACT.Sigmoid)
-            state[(gate, a)] = s
+            state["s"] = s
 
         def ep_cnext(a):
             cols = slice(a * NCOL, (a + 1) * NCOL)
             t = ep.tile([P, NCOL], F32, name="fc", tag="fc")
-            nc.vector.tensor_tensor(out=t[:], in0=state[(0, a)][:], in1=c_sb[:, cols], op=ALU.mult)
+            nc.vector.tensor_tensor(out=t[:], in0=state["s"][:], in1=c_sb[:, cols], op=ALU.mult)
             nc.vector.tensor_tensor(
                 out=natural(cn_all[:, cols]),
                 in0=natural(t[:]),
@@ -305,32 +342,28 @@ def tile_naivelstm_pb_kernel(
 
         def ep_tanh(a):
             cols = slice(a * NCOL, (a + 1) * NCOL)
-            store(out_1[:, cols], cn_all[:, cols])
+            if a == 3:
+                store(out_1, cn_all[:])
             th[a] = ep.tile([P, NCOL], F32, name="th", tag="th")
             nc.scalar.activation(out=th[a][:], in_=cn_all[:, cols], func=ACT.Tanh)
 
         def ep_hnext(a):
             cols = slice(a * NCOL, (a + 1) * NCOL)
-            nc.vector.tensor_tensor(out=hn_all[:, cols], in0=state[(1, a)][:], in1=th[a][:], op=ALU.mult)
-            store(out_0[:, cols], hn_all[:, cols])
-
-        def keep_zpart():
-            state["zpart"] = state["z"]
+            nc.vector.tensor_tensor(out=hn_all[:, cols], in0=state["s"][:], in1=th[a][:], op=ALU.mult)
+            if a == 2:
+                store(out_0[:, 0 : 3 * NCOL], hn_all[:, 0 : 3 * NCOL])
 
         def schedule_epilogue(slot, ci):
             wsel, a = CHUNKS[ci]
             if wsel == 1:
                 defer(slot + 1, lambda: ep_z(a, 0))
-                defer(slot + 3, lambda: ep_sig(a, 0))
-                defer(max(slot + 5, C_AT), lambda: ep_cnext(a))
-                defer(max(slot + 7, C_AT + 2), lambda: ep_tanh(a))
+                defer(slot + 2, ep_sig)
+                defer(slot + 3, lambda: ep_cnext(a))
+                defer(slot + 4, lambda: ep_tanh(a))
             if wsel == 3:
                 defer(slot + 1, lambda: ep_z(a, 1))
-                defer(slot + 3, lambda: ep_sig(a, 1))
-                defer(max(slot + 5, C_AT + 4), lambda: ep_hnext(a))
-            if (wsel, a) == (2, 3):
-                defer(slot + 1, lambda: ep_z(a, 1))
-                defer(slot + 1, keep_zpart)
+                defer(slot + 2, ep_sig)
+                defer(slot + 3, lambda: ep_hnext(a))
 
         def last_z(j):
             zl = ep.tile([P, P], F32, name="zl", tag="zl", bufs=4)
@@ -349,83 +382,54 @@ def tile_naivelstm_pb_kernel(
             nc.vector.tensor_tensor(
                 out=hn_all[:, cols], in0=state["sl%d" % j][:], in1=th[3][:, j * P : (j + 1) * P], op=ALU.mult
             )
-            store(out_0[:, cols], hn_all[:, cols])
+            if j == 2:
+                store(out_0[:, 3 * NCOL : 3 * NCOL + 3 * P], hn_all[:, 3 * NCOL : 3 * NCOL + 3 * P])
+            if j == 3:
+                store(out_0[:, cols], hn_all[:, cols])
 
-        def loads_after(n):
-            ci, r = divmod(n, 8)
-            if ci < LAST and r % 4 == 3:
-                done = 2 * ci + r // 4
-            elif ci == LAST and r % 2 == 1:
-                done = 2 * LAST + r // 2
-            else:
-                return
-            if done >= 1 and done + WBUFS < NLOADS:
-                load(done + WBUFS)
-
-        NMAIN = 8 * LAST
-        xg = None
-        hgs = None
-        for n in range(NMAIN):
-            unit_t(n, "V" if n % 16 in V_COPIES else "S")
-            loads_after(n)
-            if n == X_AT:
-                xg = prepare_x()
-            if n == X_AT + 2:
-                quantise(xg, act_codes[0][:], act_scales[0][:])
-            if n == H_AT:
-                hgs = prepare_h()
-            if n == H_AT + 2:
-                for gp in range(2):
-                    cols = slice(gp * 256, (gp + 1) * 256)
-                    quantise(hgs[gp], act_codes[1][:, cols], act_scales[1][:, cols])
-            if n == IG_AT:
+        for k in range(NMAIN):
+            unit_t(k)
+            loads_after(k)
+            if k >= 1:
+                unit_q(k - 1)
+            if k == X_AT:
+                prepare_x()
+            if k == H_AT:
+                prepare_h()
+            if k == X_AT + 1:
+                quantise_act(0)
+            if k == H_AT + 1:
+                quantise_act(1)
+            if k == IG_AT:
                 prepare_ig()
-            for i in range(8):
-                if BIAS_AT[i] == n:
-                    spread_bias(i % 2, i // 2)
-            if n >= QLAG:
-                unit_q(n - QLAG)
-            m = n - MXLAG
-            if m >= 0 and m % 8 == 7:
-                chunk_mx(m // 8)
-                schedule_epilogue(n, m // 8)
-            for fn in deferred.get(n, []):
-                fn()
+            for n in range(8):
+                if BIAS_AT[n] == k:
+                    spread_bias(n % 2, n // 2)
+            if k % 2 == 1 and k >= 3:
+                chunk_mx((k - 3) // 2)
+                schedule_epilogue(k, (k - 3) // 2)
+            late(k)
 
-        def block_t(j):
-            for s in range(2):
-                unit_t(NMAIN + 2 * j + s, "SS"[s])
-                loads_after(NMAIN + 2 * j + s)
-
-        def late(n):
-            for fn in deferred.get(n, []):
-                fn()
-
-        block_t(0)
-        unit_q(NMAIN - 2)
+        unit_t(NMAIN, "SS")
+        loads_after(NMAIN)
         unit_q(NMAIN - 1)
         late(NMAIN)
-        late(NMAIN + 1)
-        block_t(1)
+        unit_t(NMAIN + 1, "SS")
+        loads_after(NMAIN + 1)
         unit_q(NMAIN)
+        chunk_mx(LAST - 1)
+        late(NMAIN + 1)
+        unit_t(NMAIN + 2, "SS")
         unit_q(NMAIN + 1)
         late(NMAIN + 2)
-        late(NMAIN + 3)
-        chunk_mx(LAST - 1)
-        block_t(2)
-        unit_q(NMAIN + 2)
-        unit_q(NMAIN + 3)
-        late(NMAIN + 4)
-        late(NMAIN + 5)
         ep_z(3, 1)
-        keep_zpart()
-        block_t(3)
-        unit_q(NMAIN + 4)
-        unit_q(NMAIN + 5)
+        state["zpart"] = state["z"]
+        unit_t(NMAIN + 3, "SS")
+        unit_q(NMAIN + 2)
+        late(NMAIN + 3)
         for j in range(3):
             block_mx(j)
-        unit_q(NMAIN + 6)
-        unit_q(NMAIN + 7)
+        unit_q(NMAIN + 3)
         block_mx(3)
         for j in range(3):
             last_z(j)

from contextlib import ExitStack

import concourse.mybir as mybir
from concourse.masks import make_identity

F32 = mybir.dt.float32
BF16 = mybir.dt.bfloat16
U32 = mybir.dt.uint32
U8 = mybir.dt.uint8
I32 = mybir.dt.int32
FP8X4 = mybir.dt.float8_e4m3fn_x4
ACT = mybir.ActivationFunctionType
ALU = mybir.AluOpType

P = 128
K = 2048
HID = 2048
NCOL = 512
WBUFS = 6
V_BANKS = (1, 5)
V_BANKS_EARLY = (1, 5)
EARLY_UNITS = 6
SPLIT_CHUNKS = ()
BIAS_AT = (2, 2, 3, 3, 4, 4, 5, 5)
X_AT = 1
H_AT = 2
IG_AT = 4

FLOPS = 2 * 4 * 2048 * 2048 * 128

CHUNKS = (
    (0, 0), (1, 0), (2, 0), (3, 0),
    (0, 1), (1, 1), (2, 1), (3, 1),
    (0, 2), (1, 2), (0, 3), (1, 3),
    (2, 2), (3, 2), (2, 3), (3, 3),
)
ACC_BANK = {(0, 0): 0, (1, 0): 1, (0, 1): 0, (1, 1): 1, (0, 2): 0, (0, 3): 1, (1, 2): 0, (1, 3): 1}
LAST = len(CHUNKS) - 1


def tile_naivelstm_pb_kernel(
    tc, x, h, c, ig, w_if, w_io, w_hf, w_ho, b_if, b_hf, b_io, b_ho, out_0, out_1
):
    nc = tc.nc
    with ExitStack() as ctx:
        ctx.enter_context(tc.manual_schedule())
        const = ctx.enter_context(tc.tile_pool(name="const", bufs=1))
        wpool = ctx.enter_context(tc.tile_pool(name="wpool", bufs=WBUFS))
        gpool = ctx.enter_context(tc.tile_pool(name="gpool", bufs=3))
        cpool = ctx.enter_context(tc.tile_pool(name="cpool", bufs=6))
        ep = ctx.enter_context(tc.tile_pool(name="ep", bufs=2))
        accp = ctx.enter_context(tc.psum_pool(name="accp", bufs=1))
        tp = ctx.enter_context(tc.psum_pool(name="tp", bufs=6))

        weights = (w_if, w_hf, w_io, w_ho)

        ident32 = const.tile([P, P], F32, name="ident32")
        identb = const.tile([P, P], BF16, name="identb")
        brows = const.tile([P, NCOL], BF16, name="brows")
        nc.vector.memset(brows[:].bitcast(I32), 0)
        for first_row, b in ((0, b_if), (1, b_hf), (2, b_io), (3, b_ho)):
            nc.scalar.dma_start(
                out=brows[first_row : 16 : 4, :], in_=b.rearrange("(a n) o -> a (n o)", a=4)
            )
        make_identity(nc, identb[:])
        make_identity(nc, ident32[:])
        pairsel = const.tile([P, 8], BF16, name="pairsel")
        nc.vector.tensor_tensor(out=pairsel[:], in0=identb[:, 0:16:2], in1=identb[:, 1:16:2], op=ALU.add)
        warm = const.tile([P, 2], F32, name="warm")
        nc.vector.memset(warm[:], 0.0)
        nc.scalar.activation(out=warm[:, 1:2], in_=warm[:, 0:1], func=ACT.Sigmoid)

        loads = []
        units = []
        for ci in range(LAST):
            if ci in SPLIT_CHUNKS:
                for gp in range(2):
                    units.append((len(loads), "half", ci, gp))
                    loads.append(("half", ci, gp))
            else:
                for gp in range(2):
                    units.append((len(loads), "whole", ci, gp))
                loads.append(("whole", ci, 0))
        NMAIN = len(units)
        for j in range(4):
            units.append((len(loads), "block", LAST, j))
            loads.append(("block", LAST, j))
        last_unit_of_load = {}
        for k in range(len(units)):
            last_unit_of_load[units[k][0]] = k

        wt = {}
        stores = {"open": False, "pending": []}

        def load(n):
            kind, ci, part = loads[n]
            wsel, a = CHUNKS[ci]
            w = weights[wsel]
            if kind == "whole":
                t = wpool.tile([P, 4 * K], BF16, name="wt", tag="wt")
                nc.sync.dma_start(
                    out=t[:], in_=w.rearrange("(a q j) k -> a q (j k)", a=4, q=P, j=4)[a, :, :]
                )
            elif kind == "half":
                t = wpool.tile([P, 4, K // 2], BF16, name="wt", tag="wt")
                nc.sync.dma_start(
                    out=t[:],
                    in_=w.rearrange("(a q j) k -> a q j k", a=4, q=P, j=4)[
                        a, :, :, part * (K // 2) : (part + 1) * (K // 2)
                    ],
                )
            else:
                t = wpool.tile([P, K], BF16, name="wt", tag="wt")
                nc.sync.dma_start(out=t[:], in_=w[a * NCOL + part * P : a * NCOL + (part + 1) * P, :])
            wt[n] = t
            if n == len(loads) - 1:
                stores["open"] = True
                for dst, src in stores["pending"]:
                    nc.sync.dma_start(out=dst, in_=src)

        def store(dst, src):
            if stores["open"]:
                nc.sync.dma_start(out=dst, in_=src)
            else:
                stores["pending"].append((dst, src))

        h_sb = const.tile([P, K], BF16, name="h_sb")
        xraw = const.tile([P, 8, 2, P], BF16, name="xraw")
        ig_sb = const.tile([P, 4, 4 * P], BF16, name="ig_sb")
        c_sb = const.tile([P, HID], BF16, name="c_sb")
        load(0)
        nc.sync.dma_start(out=xraw[:], in_=x.rearrange("(s p e) b -> p s e b", s=8, p=P, e=2))
        load(1)
        nc.sync.dma_start(out=h_sb[:], in_=h)
        load(2)
        nc.sync.dma_start(out=ig_sb[:], in_=ig.rearrange("(a q j) b -> q a (j b)", a=4, q=P, j=4))
        nc.sync.dma_start(out=c_sb[:], in_=c)
        load(3)
        load(4)
        progress = {"loaded": 5, "freed": 0}

        def loads_after(k):
            if last_unit_of_load[units[k][0]] == k:
                progress["freed"] = progress["freed"] + 1
            while progress["loaded"] < len(loads) and progress["loaded"] - progress["freed"] < WBUFS:
                load(progress["loaded"])
                progress["loaded"] = progress["loaded"] + 1

        while progress["loaded"] < WBUFS:
            load(progress["loaded"])
            progress["loaded"] = progress["loaded"] + 1

        def transpose_bank(src32, cols):
            bank = tp.tile([P, 2, 2, P], F32, name="xt", tag="xt")
            for u in range(2):
                for s in range(2):
                    col = cols[u][s]
                    nc.tensor.transpose(bank[:, u, s, :], src32[:, col : col + P], ident32[:])
            return bank

        def copy_bank(eng, grouped, slot, bank):
            dst = grouped[:].bitcast(F32).rearrange("p (n u) -> p n u", u=2)
            dst = dst[:, slot * 256 : (slot + 1) * 256, :]
            src = bank[:].rearrange("p u s q -> p (s q) u")
            if eng == "S":
                nc.scalar.copy(out=dst, in_=src)
            else:
                nc.vector.tensor_copy(out=dst, in_=src)

        def row_block_cols(gp):
            return [[(2 * (2 * gp + s) + u) * P for s in range(2)] for u in range(2)]

        act_codes = []
        act_scales = []
        for nm in ("x", "h"):
            act_codes.append(const.tile([P, 512], U32, name="codes_" + nm, align_bytes=64))
            act_scales.append(const.tile([P, 512], U8, name="scales_" + nm, align_bytes=64))
        act_grouped = {}

        def prepare_x():
            xg = gpool.tile([P, K], BF16, name="grouped", tag="grouped", align_bytes=64)
            nc.vector.tensor_copy(
                out=xg[:].rearrange("p (g b t) -> p g b t", g=4, b=P, t=4),
                in_=xraw[:].rearrange("p (g u) e b -> p g b (u e)", g=4, u=2),
            )
            act_grouped[0] = xg

        def prepare_h():
            h32 = h_sb[:].bitcast(F32)
            hg = gpool.tile([P, K], BF16, name="grouped", tag="grouped", align_bytes=64)
            hbanks = [transpose_bank(h32, row_block_cols(gp)) for gp in range(2)]
            for gp in range(2):
                copy_bank("SV"[gp], hg, gp, hbanks[gp])
            act_grouped[1] = hg

        def quantise_act(opnd):
            nc.vector.quantize_mx(
                out=act_codes[opnd][:].bitcast(FP8X4), scales=act_scales[opnd][:], in_=act_grouped[opnd][:]
            )

        igT = const.tile([P, 4, 4, P], BF16, name="igT")

        def prepare_ig():
            for half in range(2):
                ibank = tp.tile([P, 2, 4, P], BF16, name="ibank", tag="xt")
                for a2 in range(2):
                    for j in range(4):
                        nc.tensor.transpose(
                            ibank[:, a2, j, :],
                            ig_sb[:, 2 * half + a2, j * P : (j + 1) * P],
                            identb[:],
                        )
                nc.scalar.copy(out=igT[:, 2 * half : 2 * half + 2, :, :], in_=ibank[:])

        bias = const.tile([P, 2 * HID], F32, name="bias")

        def spread_bias(gate, a):
            cols = slice(gate * HID + a * NCOL, gate * HID + (a + 1) * NCOL)
            bbank = tp.tile([P, NCOL], F32, name="bbank", tag="xt")
            i = 2 * a + gate
            nc.tensor.matmul(
                out=bbank[:], lhsT=pairsel[:, i : i + 1].to_broadcast([P, P]), rhs=brows[:], start=True, stop=True
            )
            nc.scalar.copy(out=bias[:, cols], in_=bbank[:])

        cn_all = const.tile([P, HID], F32, name="cn_all")
        hn_all = const.tile([P, HID], F32, name="hn_all")
        grouped = {}
        codes = {}
        scales = {}
        acc = {}
        state = {}
        th = {}
        blk = {}
        deferred = {}
        banks_done = {"n": 0}

        def defer(slot, fn):
            deferred[slot] = deferred.get(slot, []) + [fn]

        def late(slot):
            for fn in deferred.get(slot, []):
                fn()

        def unit_t(k, engines=None):
            n, kind, ci, part = units[k]
            w32 = wt[n][:]
            if kind == "half":
                w32 = w32.rearrange("p j k -> p (j k)")
            w32 = w32.bitcast(F32)
            if kind == "block":
                grouped[k] = gpool.tile([P, K], BF16, name="grouped", tag="grouped", align_bytes=64)
                colmaps = [row_block_cols(gp) for gp in range(2)]
            else:
                grouped[k] = gpool.tile([P, 2 * K], BF16, name="grouped", tag="grouped", align_bytes=64)
                rowlen = 1024 if kind == "whole" else 512
                first = 2 * part if kind == "whole" else 0
                colmaps = [
                    [[(2 * jp + s) * rowlen + (2 * (first + gg) + u) * P for s in range(2)] for u in range(2)]
                    for gg in range(2)
                    for jp in range(2)
                ]
            for slot in range(len(colmaps)):
                bank = transpose_bank(w32, colmaps[slot])
                if engines is None and k >= NMAIN - 1:
                    eng = "S"
                elif engines is None:
                    eng = "V" if banks_done["n"] % 8 in (V_BANKS_EARLY if k < EARLY_UNITS else V_BANKS) else "S"
                else:
                    eng = engines[slot]
                banks_done["n"] = banks_done["n"] + 1
                copy_bank(eng, grouped[k], slot, bank)

        def unit_q(k):
            width = NCOL if units[k][1] == "block" else 2 * NCOL
            codes[k] = cpool.tile([P, width], U32, name="codes", tag="codes", align_bytes=64)
            scales[k] = cpool.tile([P, width], U8, name="scales", tag="scales", align_bytes=64)
            nc.vector.quantize_mx(
                out=codes[k][:].bitcast(FP8X4), scales=scales[k][:], in_=grouped[k][:]
            )

        def mx(out, opnd, g, k, cols, start, stop):
            nc.tensor.matmul_mx(
                out=out,
                lhsT=act_codes[opnd][:, g * P : (g + 1) * P].bitcast(FP8X4),
                lhsT_scale=act_scales[opnd][:, g * P : (g + 1) * P],
                rhs=codes[k][:, cols].bitcast(FP8X4),
                rhs_scale=scales[k][:, cols],
                start=start,
                stop=stop,
            )

        def chunk_mx(ci):
            wsel, a = CHUNKS[ci]
            gate, opnd = divmod(wsel, 2)
            alone = (wsel, a) == (2, 3)
            if opnd == 0:
                bank = ACC_BANK[(gate, a)]
                acc[gate] = accp.tile([P, NCOL], F32, name="acc%d" % bank, tag="acc%d" % bank)
            for g in range(4):
                mx(
                    acc[gate][:], opnd, g, 2 * ci + g // 2, slice((g % 2) * NCOL, (g % 2 + 1) * NCOL),
                    opnd == 0 and g == 0, (opnd == 1 or alone) and g == 3,
                )

        def block_mx(j):
            if j == 0:
                blk[j] = accp.tile([P, P], F32, name="acc0", tag="acc0")
            else:
                blk[j] = tp.tile([P, P], F32, name="blk", tag="xt")
            for g in range(4):
                mx(blk[j][:], 1, g, NMAIN + j, slice(g * P, (g + 1) * P), g == 0, g == 3)

        def natural(ap):
            return ap.rearrange("p (q j) -> p q j", j=4)

        def ep_z(a, gate):
            z = ep.tile([P, NCOL], F32, name="z", tag="z")
            nc.vector.tensor_tensor(
                out=natural(z[:]),
                in0=acc[gate][:].rearrange("p (j q) -> p q j", j=4),
                in1=natural(bias[:, gate * HID + a * NCOL : gate * HID + (a + 1) * NCOL]),
                op=ALU.add,
            )
            state["z"] = z

        def ep_sig():
            s = ep.tile([P, NCOL], F32, name="sg", tag="sg")
            nc.scalar.activation(out=s[:], in_=state["z"][:], func=ACT.Sigmoid)
            state["s"] = s

        def ep_cnext(a):
            cols = slice(a * NCOL, (a + 1) * NCOL)
            t = ep.tile([P, NCOL], F32, name="fc", tag="fc")
            nc.vector.tensor_tensor(out=t[:], in0=state["s"][:], in1=c_sb[:, cols], op=ALU.mult)
            nc.vector.tensor_tensor(
                out=natural(cn_all[:, cols]),
                in0=natural(t[:]),
                in1=igT[:, a, :, :].rearrange("p j q -> p q j"),
                op=ALU.add,
            )

        def ep_tanh(a):
            cols = slice(a * NCOL, (a + 1) * NCOL)
            if a == 3:
                store(out_1, cn_all[:])
            th[a] = ep.tile([P, NCOL], F32, name="th", tag="th")
            nc.scalar.activation(out=th[a][:], in_=cn_all[:, cols], func=ACT.Tanh)

        def ep_hnext(a):
            cols = slice(a * NCOL, (a + 1) * NCOL)
            nc.vector.tensor_tensor(out=hn_all[:, cols], in0=state["s"][:], in1=th[a][:], op=ALU.mult)
            if a == 2:
                store(out_0[:, 0 : 3 * NCOL], hn_all[:, 0 : 3 * NCOL])

        def schedule_epilogue(slot, ci):
            wsel, a = CHUNKS[ci]
            if wsel == 1:
                defer(slot + 1, lambda: ep_z(a, 0))
                defer(slot + 2, ep_sig)
                defer(slot + 3, lambda: ep_cnext(a))
                defer(slot + 4, lambda: ep_tanh(a))
            if wsel == 3:
                defer(slot + 1, lambda: ep_z(a, 1))
                defer(slot + 2, ep_sig)
                defer(slot + 3, lambda: ep_hnext(a))

        def last_z(j):
            zl = ep.tile([P, P], F32, name="zl", tag="zl", bufs=4)
            nc.vector.tensor_tensor(
                out=zl[:], in0=blk[j][:], in1=state["zpart"][:, j * P : (j + 1) * P], op=ALU.add
            )
            state["zl%d" % j] = zl

        def last_sig(j):
            sl = ep.tile([P, P], F32, name="sl", tag="sl", bufs=4)
            nc.scalar.activation(out=sl[:], in_=state["zl%d" % j][:], func=ACT.Sigmoid)
            state["sl%d" % j] = sl

        def last_h(j):
            cols = slice(3 * NCOL + j * P, 3 * NCOL + (j + 1) * P)
            nc.vector.tensor_tensor(
                out=hn_all[:, cols], in0=state["sl%d" % j][:], in1=th[3][:, j * P : (j + 1) * P], op=ALU.mult
            )
            if j == 2:
                store(out_0[:, 3 * NCOL : 3 * NCOL + 3 * P], hn_all[:, 3 * NCOL : 3 * NCOL + 3 * P])
            if j == 3:
                store(out_0[:, cols], hn_all[:, cols])

        for k in range(NMAIN):
            unit_t(k)
            loads_after(k)
            if k >= 1:
                unit_q(k - 1)
            if k == X_AT:
                prepare_x()
            if k == H_AT:
                prepare_h()
            if k == X_AT + 1:
                quantise_act(0)
            if k == H_AT + 1:
                quantise_act(1)
            if k == IG_AT:
                prepare_ig()
            for n in range(8):
                if BIAS_AT[n] == k:
                    spread_bias(n % 2, n // 2)
            if k % 2 == 1 and k >= 3:
                chunk_mx((k - 3) // 2)
                schedule_epilogue(k, (k - 3) // 2)
            late(k)

        unit_t(NMAIN, "SS")
        loads_after(NMAIN)
        unit_q(NMAIN - 1)
        late(NMAIN)
        unit_t(NMAIN + 1, "SS")
        loads_after(NMAIN + 1)
        unit_q(NMAIN)
        chunk_mx(LAST - 1)
        late(NMAIN + 1)
        unit_t(NMAIN + 2, "SS")
        unit_q(NMAIN + 1)
        late(NMAIN + 2)
        ep_z(3, 1)
        state["zpart"] = state["z"]
        unit_t(NMAIN + 3, "SS")
        unit_q(NMAIN + 2)
        late(NMAIN + 3)
        for j in range(3):
            block_mx(j)
        unit_q(NMAIN + 3)
        block_mx(3)
        for j in range(3):
            last_z(j)
            last_sig(j)
        last_h(0)
        last_h(1)
        last_z(3)
        last_sig(3)
        last_h(2)
        last_h(3)
